import numpy as np
import ml_dtypes


def mxq(x, axis, fmt="e4m3"):
    dtype, down = {"e4m3": (ml_dtypes.float8_e4m3fn, 7), "e5m2": (ml_dtypes.float8_e5m2, 14)}[fmt]
    v = np.moveaxis(np.asarray(x, np.float32).astype(ml_dtypes.bfloat16).astype(np.float64), axis, -1)
    blocks = v.reshape(v.shape[:-1] + (-1, 32))
    amax = np.abs(blocks).max(-1, keepdims=True)
    byte = np.maximum(np.where(amax > 0, np.frexp(amax)[1] - 1 + 127, 0) - down, 1)
    scale = np.exp2(byte - 127.0)
    codes = (blocks / scale).astype(np.float32).astype(dtype).astype(np.float64)
    return np.moveaxis((codes * scale).reshape(v.shape), -1, axis)


WIDE = False


def mx_kscale(k):
    if not WIDE:
        return np.ones(k)
    levels = np.array([10, -10, 5, -5, 0])
    if k % 512:
        return np.exp2(np.random.permutation(np.resize(levels, k // 32))).repeat(32)
    a = np.empty((k // 512, 16))
    for p in range(k // 512):
        a[p, :8] = np.random.permutation(np.resize(levels, 8))
        for g in range(8):
            far = levels[np.abs(levels - a[p, g]) >= 10]
            a[p, g + 8] = far[np.random.randint(len(far))]
    return np.exp2(a.ravel()).repeat(32)


BF16 = ml_dtypes.bfloat16


def bf(x):
    return np.asarray(x, np.float32).astype(BF16)


def f64(x):
    return np.asarray(x).astype(np.float64)


B, N, G, L = 1024, 512, 128, 768
N2 = 2 * N
L2 = 2 * L
L_LIMIT = 1.0


def relu(v):
    return np.maximum(v, 0.0)


def setup_inputs():
    s, t = mx_kscale(N2), mx_kscale(L2)
    return {
        "Volt": bf(np.random.standard_normal((B, N2)) * s),
        "IM": bf(np.random.standard_normal((L2, N2)) / np.sqrt(N2) / s[None, :] * t[:, None]),
        "Ybr": bf(np.random.standard_normal((L2, L2)) / np.sqrt(L2) / t[None, :]),
        "n_o_mu_i_u": bf(np.random.standard_normal((B, L))),
    }


def reference(Volt, IM, Ybr, n_o_mu_i_u):
    mu = f64(n_o_mu_i_u)
    dv = mxq(f64(Volt), 1, "e4m3") @ mxq(f64(IM), 1, "e4m3").T
    Ibr = mxq(dv, 1, "e4m3") @ mxq(f64(Ybr), 1, "e4m3").T
    i_up = Ibr[:, :L] ** 2 + Ibr[:, L:] ** 2 - L_LIMIT ** 2
    out = np.sum(relu(i_up), axis=1)
    out = out + np.sum(np.abs(mu * i_up), axis=1)
    out = out + np.sum(relu(-mu), axis=1)
    return out

@@ -1,0 +1,313 @@
+from contextlib import ExitStack
+
+import concourse.mybir as mybir
+from concourse.masks import make_identity
+
+F32 = mybir.dt.float32
+BF16 = mybir.dt.bfloat16
+U32 = mybir.dt.uint32
+U8 = mybir.dt.uint8
+I32 = mybir.dt.int32
+FP8X4 = mybir.dt.float8_e4m3fn_x4
+ALU = mybir.AluOpType
+ACT = mybir.ActivationFunctionType
+AX = mybir.AxisListType
+
+P = 128
+B, N2, L2, L = 1024, 1024, 1536, 768
+JB = B // P
+FLOPS = 2 * B * N2 * L2 + 2 * B * L2 * L2
+PIN = True
+EV = "SVSVVSSSSVVVSSSSSVSVSSSSSVVSSVSSSVSVSVSSSSVSSVSSVSSSSSSVSSSSVS"
+ABS = "SVSSSSV"
+ABS_LAST = "SSS"
+SMIN = "SSVVVSVV"
+SEQ = (
+    ("I", 0), ("I", 1), ("V", 0), ("V", 1), ("V", 2), ("V", 3), ("F"), ("S", 0, 0),
+    ("S", 0, 2), ("I", 2), ("I", 3), ("S", 0, 4), ("S", 0, 6), ("m", 2), ("I", 4), ("I", 5),
+    ("m", 0), ("m", 1), ("F"), ("S", 1, 0), ("a", 0), ("S", 1, 2), ("Y", 0, 0), ("Y", 0, 1),
+    ("Y", 0, 2), ("S", 1, 4), ("S", 1, 6), ("Y", 1, 0), ("Y", 1, 1), ("Y", 1, 2), ("F"), ("S", 2, 0),
+    ("m", 3), ("S", 2, 2), ("Y", 2, 0), ("Y", 2, 1), ("Y", 2, 2), ("S", 2, 4), ("S", 2, 6), ("m", 4),
+    ("a", 1), ("F"), ("m", 5), ("Z", 0), ("Z", 1), ("r", 0), ("r", 1), ("Z", 2),
+    ("Z", 3), ("m", 6), ("r", 2), ("m", 7), ("Z", 4), ("r", 3), ("Z", 5), ("Z", 6),
+    ("r", 6), ("r", 5), ("r", 4), ("Z", 7),
+)
+
+
+def tile_pinnlayer_pa_kernel(tc, Volt, IM, Ybr, n_o_mu_i_u, out):
+    nc = tc.nc
+    with ExitStack() as ctx:
+        if PIN:
+            ctx.enter_context(tc.manual_schedule())
+        keep = ctx.enter_context(tc.tile_pool(name="keep", bufs=1))
+        stage = ctx.enter_context(tc.tile_pool(name="stage", bufs=3))
+        epi = ctx.enter_context(tc.tile_pool(name="epi", bufs=2))
+        psum = ctx.enter_context(tc.psum_pool(name="psum", bufs=8))
+
+        ident = keep.tile([P, P], F32, name="ident")
+        make_identity(nc, ident[:])
+
+        volt_sb = keep.tile([P, JB, N2], BF16, name="volt_sb")
+        im_sb = keep.tile([P, 6, 2, N2], BF16, name="im_sb")
+        ybr_sb = keep.tile([P, 12, L2], BF16, name="ybr_sb")
+        mu_sb = keep.tile([P, JB, L], BF16, name="mu_sb")
+        a_sb = keep.tile([P, JB, L], BF16, name="a_sb")
+
+        vcodes = keep.tile([P, JB * 256], U32, name="vcodes", align_bytes=64)
+        vscales = keep.tile([P, JB * 256], U8, name="vscales", align_bytes=64)
+        icodes = keep.tile([P, 12 * 256], U32, name="icodes", align_bytes=64)
+        iscales = keep.tile([P, 12 * 256], U8, name="iscales", align_bytes=64)
+        ycodes = keep.tile([P, 3 * L2], U32, name="ycodes", align_bytes=64)
+        yscales = keep.tile([P, 3 * L2], U8, name="yscales", align_bytes=64)
+        dcodes = keep.tile([P, 3 * B], U32, name="dcodes", align_bytes=64)
+        dscales = keep.tile([P, 3 * B], U8, name="dscales", align_bytes=64)
+
+        acc_s = keep.tile([P, JB, 6], F32, name="acc_s")
+        acc_v = keep.tile([P, JB, 3], F32, name="acc_v")
+        negmu_s = keep.tile([P, JB], F32, name="negmu_s")
+        negmu_v = keep.tile([P, JB], F32, name="negmu_v")
+        warm = keep.tile([P, 1], F32, name="warm")
+        nc.vector.memset(warm[:], 0.0)
+        nc.vector.memset(acc_s[:], 0.0)
+        nc.vector.memset(acc_v[:], 0.0)
+        nc.vector.memset(negmu_s[:], 0.0)
+        nc.vector.memset(negmu_v[:], 0.0)
+        nc.scalar.activation(out=warm[:], in_=warm[:], func=ACT.Abs)
+
+        volt_v = Volt.rearrange("(p j) k -> p j k", j=JB)
+        im_v = IM.rearrange("(g p e) k -> p g e k", g=3, e=4)
+        ybr_v = Ybr.rearrange("(r p) k -> p r k", p=P)
+        mu_v = n_o_mu_i_u.rearrange("(p j) l -> p j l", j=JB)
+
+        def load_im(t):
+            nc.sync.dma_start(out=im_sb[:, t, :, :], in_=im_v[:, t // 2, 2 * (t % 2):2 * (t % 2) + 2, :])
+
+        def load_volt(c):
+            nc.sync.dma_start(out=volt_sb[:, 2 * c:2 * c + 2, :], in_=volt_v[:, 2 * c:2 * c + 2, :])
+
+        def load_ybr(rp):
+            nc.sync.dma_start(out=ybr_sb[:, 2 * rp:2 * rp + 2, :], in_=ybr_v[:, 2 * rp:2 * rp + 2, :])
+
+        load_im(0)
+        load_im(1)
+        for c in range(4):
+            load_volt(c)
+        for t in range(2, 6):
+            load_im(t)
+        def load_mu(h):
+            nc.sync.dma_start(out=mu_sb[:, 4 * h:4 * h + 4, :], in_=mu_v[:, 4 * h:4 * h + 4, :])
+
+        load_mu(0)
+        for rp in (0, 3, 1, 4, 2, 5):
+            load_ybr(rp)
+        load_mu(1)
+
+        volt_w = volt_sb[:].bitcast(F32)
+        im_w = im_sb[:].bitcast(F32)
+        ybr_w = ybr_sb[:].bitcast(F32)
+
+        late = []
+        mark = {"done": 0, "ev": 0}
+
+        def flush(upto):
+            for k in range(mark["done"], upto):
+                late[k]()
+            mark["done"] = max(mark["done"], upto)
+
+        def evac(dst, src):
+            eng = EV[mark["ev"]]
+            mark["ev"] += 1
+            if eng == "V":
+                nc.vector.tensor_copy(out=dst, in_=src)
+            else:
+                nc.scalar.copy(out=dst, in_=src)
+
+        def quantise(codes, scales, lo, words, src):
+            def go():
+                nc.vector.quantize_mx(
+                    out=codes[:, lo:lo + words].bitcast(FP8X4),
+                    scales=scales[:, lo:lo + words],
+                    in_=src,
+                )
+            late.append(go)
+            flush(len(late) - 1)
+
+        def transposes(srcs, codes, scales, lo):
+            grouped = stage.tile([P, 2, 1024], BF16, name="grouped", align_bytes=64)
+            gw = grouped[:].bitcast(F32)
+            for h in range(2):
+                bank = psum.tile([P, 512], F32, name="bank")
+                for q in range(4):
+                    nc.tensor.transpose(bank[:, 128 * q:128 * q + 128], srcs[h][q], ident[:])
+                evac(
+                    gw[:, h, :].rearrange("p (s r u) -> p s r u", s=2, u=2),
+                    bank[:].rearrange("p (s u r) -> p s r u", s=2, u=2),
+                )
+            quantise(codes, scales, lo, 512, grouped[:].rearrange("p h c -> p (h c)"))
+
+        def every_2nd(g, u):
+            return slice(256 * g + u, 256 * g + 256, 2)
+
+        def t_volt(c):
+            srcs = [[volt_w[:, 2 * c + h, every_2nd(q // 2, q % 2)] for q in range(4)] for h in range(2)]
+            transposes(srcs, vcodes, vscales, 512 * c)
+
+        def t_im(t):
+            srcs = [[im_w[:, t, h, every_2nd(q // 2, q % 2)] for q in range(4)] for h in range(2)]
+            transposes(srcs, icodes, iscales, 512 * t)
+
+        def t_ybr(c, g):
+            srcs = [
+                [ybr_w[:, 2 * rp + q // 2, every_2nd(g, q % 2)] for q in range(4)]
+                for rp in (c, 3 + c)
+            ]
+            transposes(srcs, ycodes, yscales, L2 * g + 512 * c)
+
+        def stage1(g2, j0):
+            dgrp = stage.tile([P, 2, 512], BF16, name="dgrp", align_bytes=64)
+            for h in range(2):
+                j = j0 + h
+                bank = psum.tile([P, 512], F32, name="bank")
+                for t in range(4):
+                    for g in range(2):
+                        wi = 256 * (4 * g2 + t) + 128 * g
+                        wv = 256 * j + 128 * g
+                        nc.tensor.matmul_mx(
+                            out=bank[:, 128 * t:128 * t + 128],
+                            lhsT=icodes[:, wi:wi + 128].bitcast(FP8X4),
+                            lhsT_scale=iscales[:, wi:wi + 128],
+                            rhs=vcodes[:, wv:wv + 128].bitcast(FP8X4),
+                            rhs_scale=vscales[:, wv:wv + 128],
+                            start=(g == 0),
+                            stop=(g == 1),
+                        )
+                evac(
+                    dgrp[:, h, :].rearrange("p (b t) -> p b t", t=4),
+                    bank[:].rearrange("p (t b) -> p b t", t=4),
+                )
+            quantise(dcodes, dscales, B * g2 + 128 * j0, 256, dgrp[:].rearrange("p h c -> p (h c)"))
+
+        def abs_mu(h):
+            nc.vector.tensor_single_scalar(
+                out=a_sb[:, 4 * h:4 * h + 4, :].bitcast(I32),
+                in_=mu_sb[:, 4 * h:4 * h + 4, :].bitcast(I32),
+                scalar=0x7FFF7FFF,
+                op=ALU.bitwise_and,
+            )
+
+        def sum_neg_mu(j):
+            if SMIN[j] == "V":
+                junk_b = epi.tile([P, L], BF16, name="junk_b", bufs=1)
+                nc.vector.tensor_scalar(
+                    out=junk_b[:], in0=mu_sb[:, j, :], scalar1=0.0, scalar2=None,
+                    op0=ALU.min, op1=ALU.add, accum_out=negmu_v[:, j:j + 1],
+                )
+            else:
+                junk_s = epi.tile([P, L], F32, name="junk_s", bufs=1)
+                nc.scalar.activation(
+                    out=junk_s[:], in_=mu_sb[:, j, :], func=ACT.Relu, scale=-1.0,
+                    accum_out=negmu_s[:, j:j + 1],
+                )
+
+        ys = {}
+
+        def abs_sum(j, lo, hi, eng, col):
+            y = ys[j]
+            if eng == "V":
+                junk_v = epi.tile([P, L], F32, name="junk_v", bufs=1)
+                nc.vector.scalar_tensor_tensor(
+                    out=junk_v[:, lo:hi], in0=y[:, lo:hi], scalar=-1.0, in1=y[:, lo:hi],
+                    op0=ALU.mult, op1=ALU.max, accum_out=acc_v[:, j, col:col + 1],
+                )
+            else:
+                junk_s = epi.tile([P, L], F32, name="junk_s", bufs=1)
+                nc.scalar.activation(
+                    out=junk_s[:, lo:hi], in_=y[:, lo:hi], func=ACT.Abs, scale=2.0,
+                    accum_out=acc_s[:, j, 3 + col:4 + col],
+                )
+
+        def xy(j, sq, x, y, lo, hi):
+            nc.vector.scalar_tensor_tensor(
+                out=x[:, lo:hi], in0=sq[:, 0, lo:hi], scalar=-1.0, in1=sq[:, 1, lo:hi],
+                op0=ALU.add, op1=ALU.add,
+            )
+            nc.vector.scalar_tensor_tensor(
+                out=y[:, lo:hi], in0=a_sb[:, j, lo:hi], scalar=0.5, in1=x[:, lo:hi],
+                op0=ALU.add, op1=ALU.mult,
+            )
+
+        def stage2(j):
+            flush(len(late))
+            last = j == JB - 1
+            sq = epi.tile([P, 2, L], F32, name="sq", bufs=3)
+            x = epi.tile([P, L], F32, name="x")
+            y = epi.tile([P, L], F32, name="y", bufs=4)
+            ys[j] = y
+            for c in range(3):
+                bank = psum.tile([P, 512], F32, name="bank")
+                for g in range(3):
+                    wd = B * g + 128 * j
+                    wy = L2 * g + 512 * c
+                    nc.tensor.matmul_mx(
+                        out=bank[:],
+                        lhsT=dcodes[:, wd:wd + 128].bitcast(FP8X4),
+                        lhsT_scale=dscales[:, wd:wd + 128],
+                        rhs=ycodes[:, wy:wy + 512].bitcast(FP8X4),
+                        rhs_scale=yscales[:, wy:wy + 512],
+                        start=(g == 0),
+                        stop=(g == 2),
+                    )
+                nc.scalar.activation(
+                    out=sq[:, :, 256 * c:256 * c + 256],
+                    in_=bank[:].rearrange("p (a w) -> p a w", a=2),
+                    func=ACT.Square,
+                    accum_out=acc_s[:, j, c:c + 1],
+                )
+                if last:
+                    xy(j, sq, x, y, 256 * c, 256 * c + 256)
+                    if c > 0:
+                        abs_sum(j, 256 * (c - 1), 256 * c, ABS_LAST[c - 1], c - 1)
+            if last:
+                abs_sum(j, 512, 768, ABS_LAST[2], 2)
+            else:
+                xy(j, sq, x, y, 0, L)
+
+        for tok in SEQ:
+            kind = tok[0]
+            args = tok[1:]
+            if kind == "I":
+                t_im(args[0])
+            elif kind == "V":
+                t_volt(args[0])
+            elif kind == "Y":
+                t_ybr(args[0], args[1])
+            elif kind == "S":
+                stage1(args[0], args[1])
+            elif kind == "F":
+                flush(len(late))
+            elif kind == "a":
+                abs_mu(args[0])
+            elif kind == "m":
+                sum_neg_mu(args[0])
+            elif kind == "Z":
+                stage2(args[0])
+            elif kind == "r":
+                abs_sum(args[0], 0, L, ABS[args[0]], 0)
+
+        base = keep.tile([P, JB], F32, name="base")
+        nc.vector.tensor_scalar(
+            out=base[:], in0=negmu_v[:], scalar1=-1.0, scalar2=-0.5 * L, op0=ALU.mult, op1=ALU.add,
+        )
+        base2 = keep.tile([P, JB], F32, name="base2")
+        nc.vector.tensor_add(out=base2[:], in0=base[:], in1=negmu_s[:])
+        rv = keep.tile([P, JB], F32, name="rv")
+        nc.vector.tensor_reduce(out=rv[:], in_=acc_v[:], axis=AX.X, op=ALU.add)
+        pre = keep.tile([P, JB], F32, name="pre")
+        nc.vector.tensor_add(out=pre[:], in0=rv[:], in1=base2[:])
+        rs = keep.tile([P, JB], F32, name="rs")
+        nc.vector.tensor_reduce(out=rs[:], in_=acc_s[:], axis=AX.X, op=ALU.add)
+        res = keep.tile([P, JB], F32, name="res")
+        nc.vector.scalar_tensor_tensor(
+            out=res[:], in0=rs[:], scalar=0.5, in1=pre[:], op0=ALU.mult, op1=ALU.add,
+        )
+        nc.sync.dma_start(out=out.rearrange("(p j) -> p j", j=JB), in_=res[:])

@@ -17,31 +17,37 @@ P = 128
 B, N2, L2, L = 1024, 1024, 1536, 768
 JB = B // P
 FLOPS = 2 * B * N2 * L2 + 2 * B * L2 * L2
-PIN = True
-EV = "SVSVVSSSSVVVSSSSSVSVSSSSSVVSSVSSSVSVSVSSSSVSSVSSVSSSSSSVSSSSVS"
-ABS = "SVSSSSV"
-ABS_LAST = "SSS"
-SMIN = "SSVVVSVV"
-SEQ = (
-    ("I", 0), ("I", 1), ("V", 0), ("V", 1), ("V", 2), ("V", 3), ("F"), ("S", 0, 0),
-    ("S", 0, 2), ("I", 2), ("I", 3), ("S", 0, 4), ("S", 0, 6), ("m", 2), ("I", 4), ("I", 5),
-    ("m", 0), ("m", 1), ("F"), ("S", 1, 0), ("a", 0), ("S", 1, 2), ("Y", 0, 0), ("Y", 0, 1),
-    ("Y", 0, 2), ("S", 1, 4), ("S", 1, 6), ("Y", 1, 0), ("Y", 1, 1), ("Y", 1, 2), ("F"), ("S", 2, 0),
-    ("m", 3), ("S", 2, 2), ("Y", 2, 0), ("Y", 2, 1), ("Y", 2, 2), ("S", 2, 4), ("S", 2, 6), ("m", 4),
-    ("a", 1), ("F"), ("m", 5), ("Z", 0), ("Z", 1), ("r", 0), ("r", 1), ("Z", 2),
-    ("Z", 3), ("m", 6), ("r", 2), ("m", 7), ("Z", 4), ("r", 3), ("Z", 5), ("Z", 6),
-    ("r", 6), ("r", 5), ("r", 4), ("Z", 7),
-)
+LEAD = 6
+RUNS = (2, 3, 3, 3, 2, 0)
+DIRECT = 4
+AHEAD = 2
+EVERY_V = 4
+ABS_V = 6
+YLAG, WLAG = 2, 3
+MU_A = {22: (-1,), 23: (0,), 24: (1,), 25: (-2,), 26: (2,), 27: (3,)}
+MU_B = {4: (4,), 7: (5,), 10: (6,), 13: (7,)}
+
+
+def unit_order():
+    turns = [("I", 0), ("I", 1)] + [("V", c) for c in range(4)] + [("I", t) for t in range(2, 6)]
+    turns = turns + [("Y", c, g) for c in range(3) for g in range(3)]
+    first = [("S", g, q) for g in range(3) for q in range(4)]
+    order = turns[:LEAD]
+    done = LEAD
+    for i, run in enumerate(RUNS):
+        order = order + first[2 * i:2 * i + 2] + turns[done:done + run]
+        done += run
+    assert done == len(turns)
+    return turns, order
 
 
 def tile_pinnlayer_pa_kernel(tc, Volt, IM, Ybr, n_o_mu_i_u, out):
     nc = tc.nc
     with ExitStack() as ctx:
-        if PIN:
-            ctx.enter_context(tc.manual_schedule())
+        ctx.enter_context(tc.manual_schedule())
         keep = ctx.enter_context(tc.tile_pool(name="keep", bufs=1))
-        stage = ctx.enter_context(tc.tile_pool(name="stage", bufs=3))
-        epi = ctx.enter_context(tc.tile_pool(name="epi", bufs=2))
+        stage = ctx.enter_context(tc.tile_pool(name="stage", bufs=4))
+        epi = ctx.enter_context(tc.tile_pool(name="epi", bufs=4))
         psum = ctx.enter_context(tc.psum_pool(name="psum", bufs=8))
 
         ident = keep.tile([P, P], F32, name="ident")
@@ -63,15 +69,12 @@ def tile_pinnlayer_pa_kernel(tc, Volt, IM, Ybr, n_o_mu_i_u, out):
         dscales = keep.tile([P, 3 * B], U8, name="dscales", align_bytes=64)
 
         acc_s = keep.tile([P, JB, 6], F32, name="acc_s")
-        acc_v = keep.tile([P, JB, 3], F32, name="acc_v")
-        negmu_s = keep.tile([P, JB], F32, name="negmu_s")
-        negmu_v = keep.tile([P, JB], F32, name="negmu_v")
+        acc_v = keep.tile([P, JB, 6], F32, name="acc_v")
+        acc_m = keep.tile([P, JB], F32, name="acc_m")
         warm = keep.tile([P, 1], F32, name="warm")
         nc.vector.memset(warm[:], 0.0)
         nc.vector.memset(acc_s[:], 0.0)
         nc.vector.memset(acc_v[:], 0.0)
-        nc.vector.memset(negmu_s[:], 0.0)
-        nc.vector.memset(negmu_v[:], 0.0)
         nc.scalar.activation(out=warm[:], in_=warm[:], func=ACT.Abs)
 
         volt_v = Volt.rearrange("(p j) k -> p j k", j=JB)
@@ -79,94 +82,94 @@ def tile_pinnlayer_pa_kernel(tc, Volt, IM, Ybr, n_o_mu_i_u, out):
         ybr_v = Ybr.rearrange("(r p) k -> p r k", p=P)
         mu_v = n_o_mu_i_u.rearrange("(p j) l -> p j l", j=JB)
 
-        def load_im(t):
-            nc.sync.dma_start(out=im_sb[:, t, :, :], in_=im_v[:, t // 2, 2 * (t % 2):2 * (t % 2) + 2, :])
+        def load_im(t, lo, hi):
+            e0 = 2 * (t % 2)
+            nc.sync.dma_start(out=im_sb[:, t, lo:hi, :], in_=im_v[:, t // 2, e0 + lo:e0 + hi, :])
 
-        def load_volt(c):
-            nc.sync.dma_start(out=volt_sb[:, 2 * c:2 * c + 2, :], in_=volt_v[:, 2 * c:2 * c + 2, :])
-
-        def load_ybr(rp):
-            nc.sync.dma_start(out=ybr_sb[:, 2 * rp:2 * rp + 2, :], in_=ybr_v[:, 2 * rp:2 * rp + 2, :])
-
-        load_im(0)
-        load_im(1)
+        load_im(0, 0, 1)
+        load_im(0, 1, 2)
+        load_im(1, 0, 2)
         for c in range(4):
-            load_volt(c)
+            nc.sync.dma_start(out=volt_sb[:, 2 * c:2 * c + 2, :], in_=volt_v[:, 2 * c:2 * c + 2, :])
         for t in range(2, 6):
-            load_im(t)
-        def load_mu(h):
-            nc.sync.dma_start(out=mu_sb[:, 4 * h:4 * h + 4, :], in_=mu_v[:, 4 * h:4 * h + 4, :])
-
-        load_mu(0)
+            load_im(t, 0, 2)
         for rp in (0, 3, 1, 4, 2, 5):
-            load_ybr(rp)
-        load_mu(1)
+            nc.sync.dma_start(out=ybr_sb[:, 2 * rp:2 * rp + 2, :], in_=ybr_v[:, 2 * rp:2 * rp + 2, :])
+        for h in range(2):
+            nc.sync.dma_start(out=mu_sb[:, 4 * h:4 * h + 4, :], in_=mu_v[:, 4 * h:4 * h + 4, :])
 
         volt_w = volt_sb[:].bitcast(F32)
         im_w = im_sb[:].bitcast(F32)
         ybr_w = ybr_sb[:].bitcast(F32)
 
+        count = {"first": 0}
         late = []
-        mark = {"done": 0, "ev": 0}
+        ordered = {}
 
-        def flush(upto):
-            for k in range(mark["done"], upto):
-                late[k]()
-            mark["done"] = max(mark["done"], upto)
-
-        def evac(dst, src):
-            eng = EV[mark["ev"]]
-            mark["ev"] += 1
+        def copy(eng, dst, src):
             if eng == "V":
                 nc.vector.tensor_copy(out=dst, in_=src)
             else:
                 nc.scalar.copy(out=dst, in_=src)
 
+        def put_in_order(unit):
+            perm = stage.tile([P, 2, 2, 2, 128], F32, name="perm", align_bytes=64)
+            for h in range(2):
+                if unit[0] == "Y":
+                    c, g = unit[1:]
+                    r0 = 2 * (c + 3 * h)
+                    src = ybr_w[:, r0:r0 + 2, 256 * g:256 * g + 256].rearrange("p r (j u) -> p r u j", u=2)
+                elif unit[0] == "I":
+                    src = im_w[:, unit[1], h, :].rearrange("p (g j u) -> p g u j", g=2, u=2)
+                else:
+                    src = volt_w[:, 2 * unit[1] + h, :].rearrange("p (g j u) -> p g u j", g=2, u=2)
+                nc.vector.tensor_copy(out=perm[:, h, :, :, :], in_=src)
+            ordered[unit] = [[perm[:, h, q // 2, q % 2, :] for q in range(4)] for h in range(2)]
+
+        def every_2nd(unit):
+            rows = im_w[:, unit[1], :, :] if unit[0] == "I" else volt_w[:, 2 * unit[1]:2 * unit[1] + 2, :]
+            return [
+                [rows[:, h, 256 * (q // 2) + q % 2:256 * (q // 2) + 256:2] for q in range(4)] for h in range(2)
+            ]
+
         def quantise(codes, scales, lo, words, src):
             def go():
                 nc.vector.quantize_mx(
-                    out=codes[:, lo:lo + words].bitcast(FP8X4),
-                    scales=scales[:, lo:lo + words],
-                    in_=src,
+                    out=codes[:, lo:lo + words].bitcast(FP8X4), scales=scales[:, lo:lo + words], in_=src,
                 )
             late.append(go)
-            flush(len(late) - 1)
 
-        def transposes(srcs, codes, scales, lo):
+        def flush(left):
+            while len(late) > left:
+                go = late[0]
+                late.remove(go)
+                go()
+
+        def turn(unit):
+            srcs = ordered[unit] if unit in ordered else every_2nd(unit)
+            if unit[0] == "I":
+                codes, scales, lo = icodes, iscales, 512 * unit[1]
+            elif unit[0] == "V":
+                codes, scales, lo = vcodes, vscales, 512 * unit[1]
+            else:
+                codes, scales, lo = ycodes, yscales, L2 * unit[2] + 512 * unit[1]
             grouped = stage.tile([P, 2, 1024], BF16, name="grouped", align_bytes=64)
             gw = grouped[:].bitcast(F32)
             for h in range(2):
                 bank = psum.tile([P, 512], F32, name="bank")
                 for q in range(4):
                     nc.tensor.transpose(bank[:, 128 * q:128 * q + 128], srcs[h][q], ident[:])
-                evac(
+                copy(
+                    "S",
                     gw[:, h, :].rearrange("p (s r u) -> p s r u", s=2, u=2),
                     bank[:].rearrange("p (s u r) -> p s r u", s=2, u=2),
                 )
             quantise(codes, scales, lo, 512, grouped[:].rearrange("p h c -> p (h c)"))
 
-        def every_2nd(g, u):
-            return slice(256 * g + u, 256 * g + 256, 2)
-
-        def t_volt(c):
-            srcs = [[volt_w[:, 2 * c + h, every_2nd(q // 2, q % 2)] for q in range(4)] for h in range(2)]
-            transposes(srcs, vcodes, vscales, 512 * c)
-
-        def t_im(t):
-            srcs = [[im_w[:, t, h, every_2nd(q // 2, q % 2)] for q in range(4)] for h in range(2)]
-            transposes(srcs, icodes, iscales, 512 * t)
-
-        def t_ybr(c, g):
-            srcs = [
-                [ybr_w[:, 2 * rp + q // 2, every_2nd(g, q % 2)] for q in range(4)]
-                for rp in (c, 3 + c)
-            ]
-            transposes(srcs, ycodes, yscales, L2 * g + 512 * c)
-
-        def stage1(g2, j0):
+        def first_matmul(g2, jp):
             dgrp = stage.tile([P, 2, 512], BF16, name="dgrp", align_bytes=64)
             for h in range(2):
-                j = j0 + h
+                j = 2 * jp + h
                 bank = psum.tile([P, 512], F32, name="bank")
                 for t in range(4):
                     for g in range(2):
@@ -174,140 +177,126 @@ def tile_pinnlayer_pa_kernel(tc, Volt, IM, Ybr, n_o_mu_i_u, out):
                         wv = 256 * j + 128 * g
                         nc.tensor.matmul_mx(
                             out=bank[:, 128 * t:128 * t + 128],
-                            lhsT=icodes[:, wi:wi + 128].bitcast(FP8X4),
-                            lhsT_scale=iscales[:, wi:wi + 128],
-                            rhs=vcodes[:, wv:wv + 128].bitcast(FP8X4),
-                            rhs_scale=vscales[:, wv:wv + 128],
-                            start=(g == 0),
-                            stop=(g == 1),
+                            lhsT=icodes[:, wi:wi + 128].bitcast(FP8X4), lhsT_scale=iscales[:, wi:wi + 128],
+                            rhs=vcodes[:, wv:wv + 128].bitcast(FP8X4), rhs_scale=vscales[:, wv:wv + 128],
+                            start=(g == 0), stop=(g == 1),
                         )
-                evac(
+                count["first"] += 1
+                copy(
+                    "V" if count["first"] % EVERY_V == 0 else "S",
                     dgrp[:, h, :].rearrange("p (b t) -> p b t", t=4),
                     bank[:].rearrange("p (t b) -> p b t", t=4),
                 )
-            quantise(dcodes, dscales, B * g2 + 128 * j0, 256, dgrp[:].rearrange("p h c -> p (h c)"))
+            quantise(dcodes, dscales, B * g2 + 256 * jp, 256, dgrp[:].rearrange("p h c -> p (h c)"))
+
+        def sum_mu(j):
+            junk_m = epi.tile([P, L // 2], F32, name="junk_m", bufs=2)
+            nc.vector.scalar_tensor_tensor(
+                out=junk_m[:], in0=mu_sb[:, j, 0:L // 2], scalar=0.0, in1=mu_sb[:, j, L // 2:L],
+                op0=ALU.add, op1=ALU.add, accum_out=acc_m[:, j:j + 1],
+            )
 
         def abs_mu(h):
             nc.vector.tensor_single_scalar(
-                out=a_sb[:, 4 * h:4 * h + 4, :].bitcast(I32),
-                in_=mu_sb[:, 4 * h:4 * h + 4, :].bitcast(I32),
-                scalar=0x7FFF7FFF,
-                op=ALU.bitwise_and,
+                out=a_sb[:, 4 * h:4 * h + 4, :].bitcast(I32), in_=mu_sb[:, 4 * h:4 * h + 4, :].bitcast(I32),
+                scalar=0x7FFF7FFF, op=ALU.bitwise_and,
             )
 
-        def sum_neg_mu(j):
-            if SMIN[j] == "V":
-                junk_b = epi.tile([P, L], BF16, name="junk_b", bufs=1)
-                nc.vector.tensor_scalar(
-                    out=junk_b[:], in0=mu_sb[:, j, :], scalar1=0.0, scalar2=None,
-                    op0=ALU.min, op1=ALU.add, accum_out=negmu_v[:, j:j + 1],
-                )
+        turns, order = unit_order()
+        at = 0
+        for n, unit in enumerate(order):
+            if unit[0] == "S":
+                if order[n - 1][0] != "S":
+                    flush(0)
+                first_matmul(unit[1], unit[2])
             else:
-                junk_s = epi.tile([P, L], F32, name="junk_s", bufs=1)
-                nc.scalar.activation(
-                    out=junk_s[:], in_=mu_sb[:, j, :], func=ACT.Relu, scale=-1.0,
-                    accum_out=negmu_s[:, j:j + 1],
-                )
+                ahead = at + AHEAD
+                if DIRECT <= ahead < len(turns):
+                    put_in_order(turns[ahead])
+                at += 1
+                turn(unit)
+            flush(1)
+            for j in MU_A.get(n, ()):
+                if j < 0:
+                    abs_mu(-1 - j)
+                else:
+                    sum_mu(j)
+        flush(0)
 
-        ys = {}
+        sqs, xs, zs = {}, {}, {}
 
-        def abs_sum(j, lo, hi, eng, col):
-            y = ys[j]
-            if eng == "V":
-                junk_v = epi.tile([P, L], F32, name="junk_v", bufs=1)
+        def square(s, bank):
+            sq = epi.tile([P, 2, 256], F32, name="sq", bufs=8)
+            sqs[s] = sq
+            nc.scalar.activation(
+                out=sq[:], in_=bank[:].rearrange("p (a w) -> p a w", a=2), func=ACT.Square,
+                accum_out=acc_s[:, s // 3, s % 3:s % 3 + 1],
+            )
+
+        def make_x(s):
+            x = epi.tile([P, 256], F32, name="x")
+            xs[s] = x
+            nc.vector.scalar_tensor_tensor(
+                out=x[:], in0=sqs[s][:, 0, :], scalar=-1.0, in1=sqs[s][:, 1, :], op0=ALU.add, op1=ALU.add,
+            )
+
+        def make_abs(s):
+            j, c = s // 3, s % 3
+            x = xs[s]
+            z = epi.tile([P, 256], F32, name="z")
+            zs[s] = z
+            if s % ABS_V == 1 and s < 20:
                 nc.vector.scalar_tensor_tensor(
-                    out=junk_v[:, lo:hi], in0=y[:, lo:hi], scalar=-1.0, in1=y[:, lo:hi],
-                    op0=ALU.mult, op1=ALU.max, accum_out=acc_v[:, j, col:col + 1],
+                    out=z[:], in0=x[:], scalar=-1.0, in1=x[:], op0=ALU.mult, op1=ALU.max,
+                    accum_out=acc_v[:, j, c:c + 1],
                 )
             else:
-                junk_s = epi.tile([P, L], F32, name="junk_s", bufs=1)
-                nc.scalar.activation(
-                    out=junk_s[:, lo:hi], in_=y[:, lo:hi], func=ACT.Abs, scale=2.0,
-                    accum_out=acc_s[:, j, 3 + col:4 + col],
-                )
+                nc.scalar.activation(out=z[:], in_=x[:], func=ACT.Abs, accum_out=acc_s[:, j, 3 + c:4 + c])
 
-        def xy(j, sq, x, y, lo, hi):
+        def weigh(s):
+            j, c = s // 3, s % 3
+            junk_w = epi.tile([P, 256], F32, name="junk_w", bufs=3)
             nc.vector.scalar_tensor_tensor(
-                out=x[:, lo:hi], in0=sq[:, 0, lo:hi], scalar=-1.0, in1=sq[:, 1, lo:hi],
-                op0=ALU.add, op1=ALU.add,
-            )
-            nc.vector.scalar_tensor_tensor(
-                out=y[:, lo:hi], in0=a_sb[:, j, lo:hi], scalar=0.5, in1=x[:, lo:hi],
-                op0=ALU.add, op1=ALU.mult,
+                out=junk_w[:], in0=zs[s][:], scalar=0.5, in1=a_sb[:, j, 256 * c:256 * c + 256],
+                op0=ALU.add, op1=ALU.mult, accum_out=acc_v[:, j, 3 + c:4 + c],
             )
 
-        def stage2(j):
-            flush(len(late))
-            last = j == JB - 1
-            sq = epi.tile([P, 2, L], F32, name="sq", bufs=3)
-            x = epi.tile([P, L], F32, name="x")
-            y = epi.tile([P, L], F32, name="y", bufs=4)
-            ys[j] = y
-            for c in range(3):
+        banks = 3 * JB
+        for s in range(banks + WLAG):
+            if s < banks:
+                j, c = s // 3, s % 3
                 bank = psum.tile([P, 512], F32, name="bank")
                 for g in range(3):
                     wd = B * g + 128 * j
                     wy = L2 * g + 512 * c
                     nc.tensor.matmul_mx(
                         out=bank[:],
-                        lhsT=dcodes[:, wd:wd + 128].bitcast(FP8X4),
-                        lhsT_scale=dscales[:, wd:wd + 128],
-                        rhs=ycodes[:, wy:wy + 512].bitcast(FP8X4),
-                        rhs_scale=yscales[:, wy:wy + 512],
-                        start=(g == 0),
-                        stop=(g == 2),
+                        lhsT=dcodes[:, wd:wd + 128].bitcast(FP8X4), lhsT_scale=dscales[:, wd:wd + 128],
+                        rhs=ycodes[:, wy:wy + 512].bitcast(FP8X4), rhs_scale=yscales[:, wy:wy + 512],
+                        start=(g == 0), stop=(g == 2),
                     )
-                nc.scalar.activation(
-                    out=sq[:, :, 256 * c:256 * c + 256],
-                    in_=bank[:].rearrange("p (a w) -> p a w", a=2),
-                    func=ACT.Square,
-                    accum_out=acc_s[:, j, c:c + 1],
-                )
-                if last:
-                    xy(j, sq, x, y, 256 * c, 256 * c + 256)
-                    if c > 0:
-                        abs_sum(j, 256 * (c - 1), 256 * c, ABS_LAST[c - 1], c - 1)
-            if last:
-                abs_sum(j, 512, 768, ABS_LAST[2], 2)
-            else:
-                xy(j, sq, x, y, 0, L)
+                square(s, bank)
+                make_x(s)
+            if 0 <= s - YLAG < banks:
+                make_abs(s - YLAG)
+            if 0 <= s - WLAG < banks:
+                weigh(s - WLAG)
+            for q in MU_B.get(s, ()):
+                sum_mu(q)
 
-        for tok in SEQ:
-            kind = tok[0]
-            args = tok[1:]
-            if kind == "I":
-                t_im(args[0])
-            elif kind == "V":
-                t_volt(args[0])
-            elif kind == "Y":
-                t_ybr(args[0], args[1])
-            elif kind == "S":
-                stage1(args[0], args[1])
-            elif kind == "F":
-                flush(len(late))
-            elif kind == "a":
-                abs_mu(args[0])
-            elif kind == "m":
-                sum_neg_mu(args[0])
-            elif kind == "Z":
-                stage2(args[0])
-            elif kind == "r":
-                abs_sum(args[0], 0, L, ABS[args[0]], 0)
-
-        base = keep.tile([P, JB], F32, name="base")
-        nc.vector.tensor_scalar(
-            out=base[:], in0=negmu_v[:], scalar1=-1.0, scalar2=-0.5 * L, op0=ALU.mult, op1=ALU.add,
-        )
-        base2 = keep.tile([P, JB], F32, name="base2")
-        nc.vector.tensor_add(out=base2[:], in0=base[:], in1=negmu_s[:])
-        rv = keep.tile([P, JB], F32, name="rv")
-        nc.vector.tensor_reduce(out=rv[:], in_=acc_v[:], axis=AX.X, op=ALU.add)
-        pre = keep.tile([P, JB], F32, name="pre")
-        nc.vector.tensor_add(out=pre[:], in0=rv[:], in1=base2[:])
-        rs = keep.tile([P, JB], F32, name="rs")
-        nc.vector.tensor_reduce(out=rs[:], in_=acc_s[:], axis=AX.X, op=ALU.add)
+        half = keep.tile([P, JB], F32, name="half")
+        nc.vector.tensor_reduce(out=half[:], in_=acc_s[:], axis=AX.X, op=ALU.add)
+        half2 = keep.tile([P, JB], F32, name="half2")
+        rest = keep.tile([P, JB], F32, name="rest")
+        nc.vector.tensor_reduce(out=half2[:], in_=acc_v[:, :, 0:3], axis=AX.X, op=ALU.add)
+        nc.vector.tensor_reduce(out=rest[:], in_=acc_v[:, :, 3:6], axis=AX.X, op=ALU.add)
+        t1 = keep.tile([P, JB], F32, name="t1")
+        nc.vector.scalar_tensor_tensor(
+            out=t1[:], in0=half2[:], scalar=-1.0 * L, in1=acc_m[:], op0=ALU.add, op1=ALU.subtract)
+        t2 = keep.tile([P, JB], F32, name="t2")
+        nc.vector.tensor_add(out=t2[:], in0=t1[:], in1=half[:])
         res = keep.tile([P, JB], F32, name="res")
         nc.vector.scalar_tensor_tensor(
-            out=res[:], in0=rs[:], scalar=0.5, in1=pre[:], op0=ALU.mult, op1=ALU.add,
+            out=res[:], in0=t2[:], scalar=0.5, in1=rest[:], op0=ALU.mult, op1=ALU.add,
         )
         nc.sync.dma_start(out=out.rearrange("(p j) -> p j", j=JB), in_=res[:])

@@ -18,14 +18,19 @@ B, N2, L2, L = 1024, 1024, 1536, 768
 JB = B // P
 FLOPS = 2 * B * N2 * L2 + 2 * B * L2 * L2
 LEAD = 6
-RUNS = (2, 3, 3, 3, 2, 0)
-DIRECT = 4
-AHEAD = 2
-EVERY_V = 4
-ABS_V = 6
-YLAG, WLAG = 2, 3
+RUNS = ((2, 2), (2, 3), (2, 3), (2, 3), (2, 2), (2, 0))
+DIRECT = 6
+AHEAD = 3
+EVERY_V = 2
+ABS_TILES = (1, 4)
+SQB = 3
+MU_END = 20
+FINE = 7
+LAST = (0, 256, 512, 768)
+FA, FW = 2, 3
+XL, AS, AV, WL = 0, 3, 2, 4
 MU_A = {22: (-1,), 23: (0,), 24: (1,), 25: (-2,), 26: (2,), 27: (3,)}
-MU_B = {4: (4,), 7: (5,), 10: (6,), 13: (7,)}
+MU_AT = {4: 4, 5: 7, 6: 10, 7: 13}
 
 
 def unit_order():
@@ -34,9 +39,12 @@ def unit_order():
     first = [("S", g, q) for g in range(3) for q in range(4)]
     order = turns[:LEAD]
     done = LEAD
-    for i, run in enumerate(RUNS):
-        order = order + first[2 * i:2 * i + 2] + turns[done:done + run]
+    at = 0
+    for mx, run in RUNS:
+        order = order + first[at:at + mx] + turns[done:done + run]
+        at += mx
         done += run
+    assert at == len(first)
     assert done == len(turns)
     return turns, order
 
@@ -68,13 +76,13 @@ def tile_pinnlayer_pa_kernel(tc, Volt, IM, Ybr, n_o_mu_i_u, out):
         dcodes = keep.tile([P, 3 * B], U32, name="dcodes", align_bytes=64)
         dscales = keep.tile([P, 3 * B], U8, name="dscales", align_bytes=64)
 
-        acc_s = keep.tile([P, JB, 6], F32, name="acc_s")
-        acc_v = keep.tile([P, JB, 6], F32, name="acc_v")
+        halves = keep.tile([P, JB, 9], F32, name="halves")
+        wholes = keep.tile([P, JB, 4], F32, name="wholes")
         acc_m = keep.tile([P, JB], F32, name="acc_m")
         warm = keep.tile([P, 1], F32, name="warm")
         nc.vector.memset(warm[:], 0.0)
-        nc.vector.memset(acc_s[:], 0.0)
-        nc.vector.memset(acc_v[:], 0.0)
+        nc.vector.memset(halves[:], 0.0)
+        nc.vector.memset(wholes[:], 0.0)
         nc.scalar.activation(out=warm[:], in_=warm[:], func=ACT.Abs)
 
         volt_v = Volt.rearrange("(p j) k -> p j k", j=JB)
@@ -94,7 +102,8 @@ def tile_pinnlayer_pa_kernel(tc, Volt, IM, Ybr, n_o_mu_i_u, out):
         for t in range(2, 6):
             load_im(t, 0, 2)
         for rp in (0, 3, 1, 4, 2, 5):
-            nc.sync.dma_start(out=ybr_sb[:, 2 * rp:2 * rp + 2, :], in_=ybr_v[:, 2 * rp:2 * rp + 2, :])
+            at = 4 * (rp % 3) + 2 * (rp // 3)
+            nc.sync.dma_start(out=ybr_sb[:, at:at + 2, :], in_=ybr_v[:, 2 * rp:2 * rp + 2, :])
         for h in range(2):
             nc.sync.dma_start(out=mu_sb[:, 4 * h:4 * h + 4, :], in_=mu_v[:, 4 * h:4 * h + 4, :])
 
@@ -102,7 +111,7 @@ def tile_pinnlayer_pa_kernel(tc, Volt, IM, Ybr, n_o_mu_i_u, out):
         im_w = im_sb[:].bitcast(F32)
         ybr_w = ybr_sb[:].bitcast(F32)
 
-        count = {"first": 0}
+        count = {"first": 0, "turn": 0}
         late = []
         ordered = {}
 
@@ -113,20 +122,23 @@ def tile_pinnlayer_pa_kernel(tc, Volt, IM, Ybr, n_o_mu_i_u, out):
                 nc.scalar.copy(out=dst, in_=src)
 
         def put_in_order(unit):
-            perm = stage.tile([P, 2, 2, 2, 128], F32, name="perm", align_bytes=64)
-            for h in range(2):
-                if unit[0] == "Y":
-                    c, g = unit[1:]
-                    r0 = 2 * (c + 3 * h)
-                    src = ybr_w[:, r0:r0 + 2, 256 * g:256 * g + 256].rearrange("p r (j u) -> p r u j", u=2)
-                elif unit[0] == "I":
-                    src = im_w[:, unit[1], h, :].rearrange("p (g j u) -> p g u j", g=2, u=2)
-                else:
-                    src = volt_w[:, 2 * unit[1] + h, :].rearrange("p (g j u) -> p g u j", g=2, u=2)
-                nc.vector.tensor_copy(out=perm[:, h, :, :, :], in_=src)
-            ordered[unit] = [[perm[:, h, q // 2, q % 2, :] for q in range(4)] for h in range(2)]
+            perm = stage.tile([P, 4, 2, 128], F32, name="perm", align_bytes=64, bufs=4)
+            if unit[0] == "Y":
+                c, g = unit[1:]
+                src = ybr_w[:, 4 * c:4 * c + 4, 256 * g:256 * g + 256].rearrange("p r (j u) -> p r u j", u=2)
+            elif unit[0] == "I":
+                src = im_w[:, unit[1], :, :].rearrange("p h (g j u) -> p (h g) u j", g=2, u=2)
+            else:
+                src = volt_w[:, 2 * unit[1]:2 * unit[1] + 2, :].rearrange("p h (g j u) -> p (h g) u j", g=2, u=2)
+            nc.vector.tensor_copy(out=perm[:], in_=src)
+            ordered[unit] = [[perm[:, 2 * h + q // 2, q % 2, :] for q in range(4)] for h in range(2)]
 
         def every_2nd(unit):
+            if unit[0] == "Y":
+                c, g = unit[1:]
+                return [
+                    [ybr_w[:, 4 * c + 2 * h + q // 2, 256 * g + q % 2:256 * g + 256:2] for q in range(4)] for h in range(2)
+                ]
             rows = im_w[:, unit[1], :, :] if unit[0] == "I" else volt_w[:, 2 * unit[1]:2 * unit[1] + 2, :]
             return [
                 [rows[:, h, 256 * (q // 2) + q % 2:256 * (q // 2) + 256:2] for q in range(4)] for h in range(2)
@@ -155,22 +167,28 @@ def tile_pinnlayer_pa_kernel(tc, Volt, IM, Ybr, n_o_mu_i_u, out):
                 codes, scales, lo = ycodes, yscales, L2 * unit[2] + 512 * unit[1]
             grouped = stage.tile([P, 2, 1024], BF16, name="grouped", align_bytes=64)
             gw = grouped[:].bitcast(F32)
+            banks = []
             for h in range(2):
                 bank = psum.tile([P, 512], F32, name="bank")
+                banks.append(bank)
                 for q in range(4):
                     nc.tensor.transpose(bank[:, 128 * q:128 * q + 128], srcs[h][q], ident[:])
+            count["turn"] += 1
+            for h in ((1, 0) if count["turn"] > 2 else (0, 1)):
                 copy(
                     "S",
                     gw[:, h, :].rearrange("p (s r u) -> p s r u", s=2, u=2),
-                    bank[:].rearrange("p (s u r) -> p s r u", s=2, u=2),
+                    banks[h][:].rearrange("p (s u r) -> p s r u", s=2, u=2),
                 )
             quantise(codes, scales, lo, 512, grouped[:].rearrange("p h c -> p (h c)"))
 
         def first_matmul(g2, jp):
             dgrp = stage.tile([P, 2, 512], BF16, name="dgrp", align_bytes=64)
+            banks = []
             for h in range(2):
                 j = 2 * jp + h
                 bank = psum.tile([P, 512], F32, name="bank")
+                banks.append(bank)
                 for t in range(4):
                     for g in range(2):
                         wi = 256 * (4 * g2 + t) + 128 * g
@@ -181,11 +199,12 @@ def tile_pinnlayer_pa_kernel(tc, Volt, IM, Ybr, n_o_mu_i_u, out):
                             rhs=vcodes[:, wv:wv + 128].bitcast(FP8X4), rhs_scale=vscales[:, wv:wv + 128],
                             start=(g == 0), stop=(g == 1),
                         )
-                count["first"] += 1
+            count["first"] += 1
+            for h in (1, 0):
                 copy(
-                    "V" if count["first"] % EVERY_V == 0 else "S",
+                    "V" if h == 0 and count["first"] % EVERY_V == 0 else "S",
                     dgrp[:, h, :].rearrange("p (b t) -> p b t", t=4),
-                    bank[:].rearrange("p (t b) -> p b t", t=4),
+                    banks[h][:].rearrange("p (t b) -> p b t", t=4),
                 )
             quantise(dcodes, dscales, B * g2 + 256 * jp, 256, dgrp[:].rearrange("p h c -> p (h c)"))
 
@@ -211,11 +230,11 @@ def tile_pinnlayer_pa_kernel(tc, Volt, IM, Ybr, n_o_mu_i_u, out):
                 first_matmul(unit[1], unit[2])
             else:
                 ahead = at + AHEAD
-                if DIRECT <= ahead < len(turns):
-                    put_in_order(turns[ahead])
                 at += 1
                 turn(unit)
             flush(1)
+            if unit[0] != "S" and DIRECT <= ahead < len(turns):
+                put_in_order(turns[ahead])
             for j in MU_A.get(n, ()):
                 if j < 0:
                     abs_mu(-1 - j)
@@ -223,80 +242,103 @@ def tile_pinnlayer_pa_kernel(tc, Volt, IM, Ybr, n_o_mu_i_u, out):
                     sum_mu(j)
         flush(0)
 
-        sqs, xs, zs = {}, {}, {}
+        im_free = im_w.rearrange("p t h w -> p (t h w)")
+        volt_free = volt_w.rearrange("p j w -> p (j w)")
+        xs, zs, sqs = {}, {}, {}
 
-        def square(s, bank):
-            sq = epi.tile([P, 2, 256], F32, name="sq", bufs=8)
-            sqs[s] = sq
-            nc.scalar.activation(
-                out=sq[:], in_=bank[:].rearrange("p (a w) -> p a w", a=2), func=ACT.Square,
-                accum_out=acc_s[:, s // 3, s % 3:s % 3 + 1],
-            )
-
-        def make_x(s):
-            x = epi.tile([P, 256], F32, name="x")
-            xs[s] = x
-            nc.vector.scalar_tensor_tensor(
-                out=x[:], in0=sqs[s][:, 0, :], scalar=-1.0, in1=sqs[s][:, 1, :], op0=ALU.add, op1=ALU.add,
-            )
-
-        def make_abs(s):
-            j, c = s // 3, s % 3
-            x = xs[s]
-            z = epi.tile([P, 256], F32, name="z")
-            zs[s] = z
-            if s % ABS_V == 1 and s < 20:
-                nc.vector.scalar_tensor_tensor(
-                    out=z[:], in0=x[:], scalar=-1.0, in1=x[:], op0=ALU.mult, op1=ALU.max,
-                    accum_out=acc_v[:, j, c:c + 1],
-                )
-            else:
-                nc.scalar.activation(out=z[:], in_=x[:], func=ACT.Abs, accum_out=acc_s[:, j, 3 + c:4 + c])
-
-        def weigh(s):
-            j, c = s // 3, s % 3
-            junk_w = epi.tile([P, 256], F32, name="junk_w", bufs=3)
-            nc.vector.scalar_tensor_tensor(
-                out=junk_w[:], in0=zs[s][:], scalar=0.5, in1=a_sb[:, j, 256 * c:256 * c + 256],
-                op0=ALU.add, op1=ALU.mult, accum_out=acc_v[:, j, 3 + c:4 + c],
-            )
-
-        banks = 3 * JB
-        for s in range(banks + WLAG):
-            if s < banks:
-                j, c = s // 3, s % 3
-                bank = psum.tile([P, 512], F32, name="bank")
+        def currents(j, lo, hi):
+            c, off, width = lo // 256, lo % 256, hi - lo
+            bank = psum.tile([P, 512], F32, name="bank")
+            parts = [(0, off, 512)] if width == 256 else [(0, off, width), (width, 256 + off, width)]
+            for to, fro, n in parts:
                 for g in range(3):
                     wd = B * g + 128 * j
-                    wy = L2 * g + 512 * c
+                    wy = L2 * g + 512 * c + fro
                     nc.tensor.matmul_mx(
-                        out=bank[:],
+                        out=bank[:, to:to + n],
                         lhsT=dcodes[:, wd:wd + 128].bitcast(FP8X4), lhsT_scale=dscales[:, wd:wd + 128],
-                        rhs=ycodes[:, wy:wy + 512].bitcast(FP8X4), rhs_scale=yscales[:, wy:wy + 512],
+                        rhs=ycodes[:, wy:wy + n].bitcast(FP8X4), rhs_scale=yscales[:, wy:wy + n],
                         start=(g == 0), stop=(g == 2),
                     )
-                square(s, bank)
-                make_x(s)
-            if 0 <= s - YLAG < banks:
-                make_abs(s - YLAG)
-            if 0 <= s - WLAG < banks:
-                weigh(s - WLAG)
-            for q in MU_B.get(s, ()):
-                sum_mu(q)
+            return bank
 
-        half = keep.tile([P, JB], F32, name="half")
-        nc.vector.tensor_reduce(out=half[:], in_=acc_s[:], axis=AX.X, op=ALU.add)
-        half2 = keep.tile([P, JB], F32, name="half2")
-        rest = keep.tile([P, JB], F32, name="rest")
-        nc.vector.tensor_reduce(out=half2[:], in_=acc_v[:, :, 0:3], axis=AX.X, op=ALU.add)
-        nc.vector.tensor_reduce(out=rest[:], in_=acc_v[:, :, 3:6], axis=AX.X, op=ALU.add)
-        t1 = keep.tile([P, JB], F32, name="t1")
-        nc.vector.scalar_tensor_tensor(
-            out=t1[:], in0=half2[:], scalar=-1.0 * L, in1=acc_m[:], op0=ALU.add, op1=ALU.subtract)
-        t2 = keep.tile([P, JB], F32, name="t2")
-        nc.vector.tensor_add(out=t2[:], in0=t1[:], in1=half[:])
+        def square(j, lo, hi, col, bank):
+            if j not in sqs:
+                sqs[j] = epi.tile([P, 2, L], F32, name="sq", bufs=SQB)
+            w = hi - lo
+            nc.scalar.activation(
+                out=sqs[j][:, :, lo:hi], in_=bank[:, 0:2 * w].rearrange("p (a w) -> p a w", a=2), func=ACT.Square,
+                accum_out=halves[:, j, col:col + 1],
+            )
+
+        def make_x(j, lo, hi):
+            if lo == 0:
+                xs[j] = im_free[:, L * (j % 4):L * (j % 4) + L]
+            nc.vector.scalar_tensor_tensor(
+                out=xs[j][:, lo:hi], in0=sqs[j][:, 0, lo:hi], scalar=-1.0, in1=sqs[j][:, 1, lo:hi], op0=ALU.add, op1=ALU.add,
+            )
+
+        def make_abs(j, lo, hi, col):
+            if lo == 0:
+                zs[j] = im_free[:, L * (4 + j % 4):L * (5 + j % 4)]
+            x, z = xs[j], zs[j]
+            if j in ABS_TILES:
+                nc.vector.scalar_tensor_tensor(
+                    out=z[:, lo:hi], in0=x[:, lo:hi], scalar=-1.0, in1=x[:, lo:hi], op0=ALU.mult, op1=ALU.max,
+                    accum_out=halves[:, j, 4 + col:5 + col],
+                )
+            else:
+                nc.scalar.activation(out=z[:, lo:hi], in_=x[:, lo:hi], func=ACT.Abs, accum_out=halves[:, j, 4 + col:5 + col])
+
+        def weigh(j, lo, hi, col):
+            junk_w = volt_free[:, L * (j % 4):L * (j % 4) + L]
+            nc.vector.scalar_tensor_tensor(
+                out=junk_w[:, lo:hi], in0=zs[j][:, lo:hi], scalar=0.5, in1=a_sb[:, j, lo:hi],
+                op0=ALU.add, op1=ALU.mult, accum_out=wholes[:, j, col:col + 1],
+            )
+
+
+        todo = {}
+
+        def after(s, f, *args):
+            todo.setdefault(s, []).append((f, args))
+
+        steps = []
+        for j in range(JB):
+            cuts = LAST if j == JB - 1 else (0, 256, 512, 768)
+            for c in range(len(cuts) - 1):
+                steps.append((j, cuts[c], cuts[c + 1], c))
+        for s in range(len(steps)):
+            j, lo, hi, c = steps[s]
+            if j < FINE:
+                if c == 2:
+                    after(s + WL, weigh, j, 0, L, 0)
+                    after(s + XL, make_x, j, 0, L)
+                    after(s + (AV if j in ABS_TILES else AS), make_abs, j, 0, L, 0)
+            else:
+                after(s, make_x, j, lo, hi)
+                after(s + FA, make_abs, j, lo, hi, c)
+                after(s + FW, weigh, j, lo, hi, c)
+        for q in range(JB):
+            if q in MU_AT:
+                after(MU_AT[q], sum_mu, q)
+        for s in range(len(steps) + 4):
+            if s < len(steps):
+                j, lo, hi, c = steps[s]
+                square(j, lo, hi, c, currents(j, lo, hi))
+            for f, args in todo.get(s, ()):
+                f(*args)
+            if s == MU_END:
+                nc.vector.tensor_scalar(
+                    out=halves[:, :, 8], in0=acc_m[:], scalar1=-1.0, scalar2=-1.0 * L, op0=ALU.mult, op1=ALU.add,
+                )
+
+        twice = keep.tile([P, JB], F32, name="twice")
+        nc.vector.tensor_reduce(out=twice[:], in_=halves[:], axis=AX.X, op=ALU.add)
+        whole = keep.tile([P, JB], F32, name="whole")
+        nc.vector.tensor_reduce(out=whole[:], in_=wholes[:], axis=AX.X, op=ALU.add)
         res = keep.tile([P, JB], F32, name="res")
         nc.vector.scalar_tensor_tensor(
-            out=res[:], in0=t2[:], scalar=0.5, in1=rest[:], op0=ALU.mult, op1=ALU.add,
+            out=res[:], in0=twice[:], scalar=0.5, in1=whole[:], op0=ALU.mult, op1=ALU.add,
         )
         nc.sync.dma_start(out=out.rearrange("(p j) -> p j", j=JB), in_=res[:])

@@ -125,12 +125,12 @@ def tile_pinnlayer_pa_kernel(tc, Volt, IM, Ybr, n_o_mu_i_u, out):
             perm = stage.tile([P, 4, 2, 128], F32, name="perm", align_bytes=64, bufs=4)
             if unit[0] == "Y":
                 c, g = unit[1:]
-                src = ybr_w[:, 4 * c:4 * c + 4, 256 * g:256 * g + 256].rearrange("p r (j u) -> p r u j", u=2)
+                src = ybr_w[:, 4 * c:4 * c + 4, 256 * g:256 * g + 256].rearrange("p r (j u) -> p r j u", u=2)
             elif unit[0] == "I":
-                src = im_w[:, unit[1], :, :].rearrange("p h (g j u) -> p (h g) u j", g=2, u=2)
+                src = im_w[:, unit[1], :, :].rearrange("p h (g j u) -> p (h g) j u", g=2, u=2)
             else:
-                src = volt_w[:, 2 * unit[1]:2 * unit[1] + 2, :].rearrange("p h (g j u) -> p (h g) u j", g=2, u=2)
-            nc.vector.tensor_copy(out=perm[:], in_=src)
+                src = volt_w[:, 2 * unit[1]:2 * unit[1] + 2, :].rearrange("p h (g j u) -> p (h g) j u", g=2, u=2)
+            nc.vector.tensor_copy(out=perm[:].rearrange("p r u j -> p r j u"), in_=src)
             ordered[unit] = [[perm[:, 2 * h + q // 2, q % 2, :] for q in range(4)] for h in range(2)]
 
         def every_2nd(unit):

@@ -18,25 +18,21 @@ B, N2, L2, L = 1024, 1024, 1536, 768
 JB = B // P
 FLOPS = 2 * B * N2 * L2 + 2 * B * L2 * L2
 LEAD = 6
-RUNS = ((2, 2), (2, 3), (2, 3), (2, 3), (2, 2), (2, 0))
+RUNS = ((1, 2), (1, 3), (1, 3), (1, 3), (1, 2), (1, 0))
 DIRECT = 6
 AHEAD = 3
-EVERY_V = 2
-ABS_TILES = (1, 4)
-SQB = 3
+ABS_TILES = [(j, 1) for j in range(0, 8, 2)]
 MU_END = 20
-FINE = 7
 LAST = (0, 256, 512, 768)
 FA, FW = 2, 3
-XL, AS, AV, WL = 0, 3, 2, 4
-MU_A = {22: (-1,), 23: (0,), 24: (1,), 25: (-2,), 26: (2,), 27: (3,)}
+MU_A = {19: (-1,), 20: (0, 1), 21: (-2,), 22: (2, 3)}
 MU_AT = {4: 4, 5: 7, 6: 10, 7: 13}
 
 
 def unit_order():
     turns = [("I", 0), ("I", 1)] + [("V", c) for c in range(4)] + [("I", t) for t in range(2, 6)]
     turns = turns + [("Y", c, g) for c in range(3) for g in range(3)]
-    first = [("S", g, q) for g in range(3) for q in range(4)]
+    first = [("S", g, q) for g in range(3) for q in range(2)]
     order = turns[:LEAD]
     done = LEAD
     at = 0
@@ -111,15 +107,9 @@ def tile_pinnlayer_pa_kernel(tc, Volt, IM, Ybr, n_o_mu_i_u, out):
         im_w = im_sb[:].bitcast(F32)
         ybr_w = ybr_sb[:].bitcast(F32)
 
-        count = {"first": 0, "turn": 0}
+        count = {"turn": 0}
         late = []
         ordered = {}
-
-        def copy(eng, dst, src):
-            if eng == "V":
-                nc.vector.tensor_copy(out=dst, in_=src)
-            else:
-                nc.scalar.copy(out=dst, in_=src)
 
         def put_in_order(unit):
             perm = stage.tile([P, 4, 2, 128], F32, name="perm", align_bytes=64, bufs=4)
@@ -175,38 +165,38 @@ def tile_pinnlayer_pa_kernel(tc, Volt, IM, Ybr, n_o_mu_i_u, out):
                     nc.tensor.transpose(bank[:, 128 * q:128 * q + 128], srcs[h][q], ident[:])
             count["turn"] += 1
             for h in ((1, 0) if count["turn"] > 2 else (0, 1)):
-                copy(
-                    "S",
-                    gw[:, h, :].rearrange("p (s r u) -> p s r u", s=2, u=2),
-                    banks[h][:].rearrange("p (s u r) -> p s r u", s=2, u=2),
+                nc.scalar.copy(
+                    out=gw[:, h, :].rearrange("p (s r u) -> p s r u", s=2, u=2),
+                    in_=banks[h][:].rearrange("p (s u r) -> p s r u", s=2, u=2),
                 )
             quantise(codes, scales, lo, 512, grouped[:].rearrange("p h c -> p (h c)"))
 
-        def first_matmul(g2, jp):
-            dgrp = stage.tile([P, 2, 512], BF16, name="dgrp", align_bytes=64)
-            banks = []
-            for h in range(2):
-                j = 2 * jp + h
-                bank = psum.tile([P, 512], F32, name="bank")
-                banks.append(bank)
-                for t in range(4):
-                    for g in range(2):
-                        wi = 256 * (4 * g2 + t) + 128 * g
-                        wv = 256 * j + 128 * g
-                        nc.tensor.matmul_mx(
-                            out=bank[:, 128 * t:128 * t + 128],
-                            lhsT=icodes[:, wi:wi + 128].bitcast(FP8X4), lhsT_scale=iscales[:, wi:wi + 128],
-                            rhs=vcodes[:, wv:wv + 128].bitcast(FP8X4), rhs_scale=vscales[:, wv:wv + 128],
-                            start=(g == 0), stop=(g == 1),
-                        )
-            count["first"] += 1
-            for h in (1, 0):
-                copy(
-                    "V" if h == 0 and count["first"] % EVERY_V == 0 else "S",
-                    dgrp[:, h, :].rearrange("p (b t) -> p b t", t=4),
-                    banks[h][:].rearrange("p (t b) -> p b t", t=4),
-                )
-            quantise(dcodes, dscales, B * g2 + 256 * jp, 256, dgrp[:].rearrange("p h c -> p (h c)"))
+        def first_matmul(g2, half):
+            dgrp = stage.tile([P, 4, 512], BF16, name="dgrp", align_bytes=64, bufs=2)
+            for pair in range(2):
+                banks = []
+                for h in range(2):
+                    j = 4 * half + 2 * pair + h
+                    bank = psum.tile([P, 512], F32, name="bank")
+                    banks.append(bank)
+                    for t in range(4):
+                        for g in range(2):
+                            wi = 256 * (4 * g2 + t) + 128 * g
+                            wv = 256 * j + 128 * g
+                            nc.tensor.matmul_mx(
+                                out=bank[:, 128 * t:128 * t + 128],
+                                lhsT=icodes[:, wi:wi + 128].bitcast(FP8X4), lhsT_scale=iscales[:, wi:wi + 128],
+                                rhs=vcodes[:, wv:wv + 128].bitcast(FP8X4), rhs_scale=vscales[:, wv:wv + 128],
+                                start=(g == 0), stop=(g == 1),
+                            )
+                for h in (1, 0):
+                    nc.scalar.copy(
+                        out=dgrp[:, 2 * pair + h, :].rearrange("p (b t) -> p b t", t=4),
+                        in_=banks[h][:].rearrange("p (t b) -> p b t", t=4),
+                    )
+                if pair == 0:
+                    flush(0)
+            quantise(dcodes, dscales, B * g2 + 512 * half, 512, dgrp[:].rearrange("p h c -> p (h c)"))
 
         def sum_mu(j):
             junk_m = epi.tile([P, L // 2], F32, name="junk_m", bufs=2)
@@ -225,8 +215,7 @@ def tile_pinnlayer_pa_kernel(tc, Volt, IM, Ybr, n_o_mu_i_u, out):
         at = 0
         for n, unit in enumerate(order):
             if unit[0] == "S":
-                if order[n - 1][0] != "S":
-                    flush(0)
+                flush(1)
                 first_matmul(unit[1], unit[2])
             else:
                 ahead = at + AHEAD
@@ -264,7 +253,7 @@ def tile_pinnlayer_pa_kernel(tc, Volt, IM, Ybr, n_o_mu_i_u, out):
 
         def square(j, lo, hi, col, bank):
             if j not in sqs:
-                sqs[j] = epi.tile([P, 2, L], F32, name="sq", bufs=SQB)
+                sqs[j] = epi.tile([P, 2, L], F32, name="sq", bufs=3)
             w = hi - lo
             nc.scalar.activation(
                 out=sqs[j][:, :, lo:hi], in_=bank[:, 0:2 * w].rearrange("p (a w) -> p a w", a=2), func=ACT.Square,
@@ -282,7 +271,7 @@ def tile_pinnlayer_pa_kernel(tc, Volt, IM, Ybr, n_o_mu_i_u, out):
             if lo == 0:
                 zs[j] = im_free[:, L * (4 + j % 4):L * (5 + j % 4)]
             x, z = xs[j], zs[j]
-            if j in ABS_TILES:
+            if (j, col) in ABS_TILES:
                 nc.vector.scalar_tensor_tensor(
                     out=z[:, lo:hi], in0=x[:, lo:hi], scalar=-1.0, in1=x[:, lo:hi], op0=ALU.mult, op1=ALU.max,
                     accum_out=halves[:, j, 4 + col:5 + col],
@@ -310,15 +299,9 @@ def tile_pinnlayer_pa_kernel(tc, Volt, IM, Ybr, n_o_mu_i_u, out):
                 steps.append((j, cuts[c], cuts[c + 1], c))
         for s in range(len(steps)):
             j, lo, hi, c = steps[s]
-            if j < FINE:
-                if c == 2:
-                    after(s + WL, weigh, j, 0, L, 0)
-                    after(s + XL, make_x, j, 0, L)
-                    after(s + (AV if j in ABS_TILES else AS), make_abs, j, 0, L, 0)
-            else:
-                after(s, make_x, j, lo, hi)
-                after(s + FA, make_abs, j, lo, hi, c)
-                after(s + FW, weigh, j, lo, hi, c)
+            after(s, make_x, j, lo, hi)
+            after(s + FA, make_abs, j, lo, hi, c)
+            after(s + FW, weigh, j, lo, hi, c)
         for q in range(JB):
             if q in MU_AT:
                 after(MU_AT[q], sum_mu, q)

@@ -19,10 +19,12 @@ JB = B // P
 FLOPS = 2 * B * N2 * L2 + 2 * B * L2 * L2
 LEAD = 6
 RUNS = ((1, 2), (1, 3), (1, 3), (1, 3), (1, 2), (1, 0))
-DIRECT = 6
+TURN_V = 3
+DIRECT = 7
 AHEAD = 3
 ABS_TILES = [(j, 1) for j in range(0, 8, 2)]
 MU_END = 20
+FINE = 5
 LAST = (0, 256, 512, 768)
 FA, FW = 2, 3
 MU_A = {19: (-1,), 20: (0, 1), 21: (-2,), 22: (2, 3)}
@@ -111,6 +113,12 @@ def tile_pinnlayer_pa_kernel(tc, Volt, IM, Ybr, n_o_mu_i_u, out):
         late = []
         ordered = {}
 
+        def copy(eng, dst, src):
+            if eng == "V":
+                nc.vector.tensor_copy(out=dst, in_=src)
+            else:
+                nc.scalar.copy(out=dst, in_=src)
+
         def put_in_order(unit):
             perm = stage.tile([P, 4, 2, 128], F32, name="perm", align_bytes=64, bufs=4)
             if unit[0] == "Y":
@@ -165,9 +173,10 @@ def tile_pinnlayer_pa_kernel(tc, Volt, IM, Ybr, n_o_mu_i_u, out):
                     nc.tensor.transpose(bank[:, 128 * q:128 * q + 128], srcs[h][q], ident[:])
             count["turn"] += 1
             for h in ((1, 0) if count["turn"] > 2 else (0, 1)):
-                nc.scalar.copy(
-                    out=gw[:, h, :].rearrange("p (s r u) -> p s r u", s=2, u=2),
-                    in_=banks[h][:].rearrange("p (s u r) -> p s r u", s=2, u=2),
+                copy(
+                    "V" if h == 0 and count["turn"] > LEAD and count["turn"] % TURN_V == 0 else "S",
+                    gw[:, h, :].rearrange("p (s r u) -> p s r u", s=2, u=2),
+                    banks[h][:].rearrange("p (s u r) -> p s r u", s=2, u=2),
                 )
             quantise(codes, scales, lo, 512, grouped[:].rearrange("p h c -> p (h c)"))
 
@@ -190,9 +199,10 @@ def tile_pinnlayer_pa_kernel(tc, Volt, IM, Ybr, n_o_mu_i_u, out):
                                 start=(g == 0), stop=(g == 1),
                             )
                 for h in (1, 0):
-                    nc.scalar.copy(
-                        out=dgrp[:, 2 * pair + h, :].rearrange("p (b t) -> p b t", t=4),
-                        in_=banks[h][:].rearrange("p (t b) -> p b t", t=4),
+                    copy(
+                        "S",
+                        dgrp[:, 2 * pair + h, :].rearrange("p (b t) -> p b t", t=4),
+                        banks[h][:].rearrange("p (t b) -> p b t", t=4),
                     )
                 if pair == 0:
                     flush(0)
@@ -301,7 +311,10 @@ def tile_pinnlayer_pa_kernel(tc, Volt, IM, Ybr, n_o_mu_i_u, out):
             j, lo, hi, c = steps[s]
             after(s, make_x, j, lo, hi)
             after(s + FA, make_abs, j, lo, hi, c)
-            after(s + FW, weigh, j, lo, hi, c)
+            if j >= FINE:
+                after(s + FW, weigh, j, lo, hi, c)
+            elif c == 2:
+                after(s + FW, weigh, j, 0, L, 0)
         for q in range(JB):
             if q in MU_AT:
                 after(MU_AT[q], sum_mu, q)

@@ -18,8 +18,8 @@ B, N2, L2, L = 1024, 1024, 1536, 768
 JB = B // P
 FLOPS = 2 * B * N2 * L2 + 2 * B * L2 * L2
 LEAD = 6
-RUNS = ((1, 2), (1, 3), (1, 3), (1, 3), (1, 2), (1, 0))
-TURN_V = 3
+RUNS = ((1, 3), (1, 3), (1, 3), (1, 2), (1, 2), (1, 0))
+TURN_V = 4
 DIRECT = 7
 AHEAD = 3
 ABS_TILES = [(j, 1) for j in range(0, 8, 2)]
@@ -27,8 +27,8 @@ MU_END = 20
 FINE = 5
 LAST = (0, 256, 512, 768)
 FA, FW = 2, 3
-MU_A = {19: (-1,), 20: (0, 1), 21: (-2,), 22: (2, 3)}
-MU_AT = {4: 4, 5: 7, 6: 10, 7: 13}
+MU_A = {19: (-1,), 20: (0,), 21: (-2, 1), 22: (2,)}
+MU_AT = {q: 3 * q - 6 for q in range(3, 8)}
 
 
 def unit_order():
@@ -58,6 +58,10 @@ def tile_pinnlayer_pa_kernel(tc, Volt, IM, Ybr, n_o_mu_i_u, out):
 
         ident = keep.tile([P, P], F32, name="ident")
         make_identity(nc, ident[:])
+        spread = keep.tile([P, P], F32, name="spread")
+        nc.vector.tensor_copy(
+            out=spread[:].rearrange("p (u q) -> p u q", u=2), in_=ident[:].rearrange("p (q u) -> p u q", u=2),
+        )
 
         volt_sb = keep.tile([P, JB, N2], BF16, name="volt_sb")
         im_sb = keep.tile([P, 6, 2, N2], BF16, name="im_sb")
@@ -84,13 +88,12 @@ def tile_pinnlayer_pa_kernel(tc, Volt, IM, Ybr, n_o_mu_i_u, out):
         nc.scalar.activation(out=warm[:], in_=warm[:], func=ACT.Abs)
 
         volt_v = Volt.rearrange("(p j) k -> p j k", j=JB)
-        im_v = IM.rearrange("(g p e) k -> p g e k", g=3, e=4)
+        im_v = IM.rearrange("(g p r e) k -> p g e r k", g=3, r=2, e=2)
         ybr_v = Ybr.rearrange("(r p) k -> p r k", p=P)
         mu_v = n_o_mu_i_u.rearrange("(p j) l -> p j l", j=JB)
 
         def load_im(t, lo, hi):
-            e0 = 2 * (t % 2)
-            nc.sync.dma_start(out=im_sb[:, t, lo:hi, :], in_=im_v[:, t // 2, e0 + lo:e0 + hi, :])
+            nc.sync.dma_start(out=im_sb[:, t, lo:hi, :], in_=im_v[:, t // 2, t % 2, lo:hi, :])
 
         load_im(0, 0, 1)
         load_im(0, 1, 2)
@@ -120,27 +123,27 @@ def tile_pinnlayer_pa_kernel(tc, Volt, IM, Ybr, n_o_mu_i_u, out):
                 nc.scalar.copy(out=dst, in_=src)
 
         def put_in_order(unit):
-            perm = stage.tile([P, 4, 2, 128], F32, name="perm", align_bytes=64, bufs=4)
+            perm = stage.tile([P, 2, 4, 128], F32, name="perm", align_bytes=64)
             if unit[0] == "Y":
                 c, g = unit[1:]
-                src = ybr_w[:, 4 * c:4 * c + 4, 256 * g:256 * g + 256].rearrange("p r (j u) -> p r j u", u=2)
-            elif unit[0] == "I":
-                src = im_w[:, unit[1], :, :].rearrange("p h (g j u) -> p (h g) j u", g=2, u=2)
+                rows = ybr_w[:, 4 * c:4 * c + 4, 256 * g:256 * g + 256]
+                pairs = rows.rearrange("p r (q u b) -> p u r q b", u=2, b=2)
+                for u in range(2):
+                    nc.vector.tensor_copy(
+                        out=perm[:, u, :, :].rearrange("p r (q b) -> p r q b", b=2), in_=pairs[:, u, :, :, :],
+                    )
             else:
-                src = volt_w[:, 2 * unit[1]:2 * unit[1] + 2, :].rearrange("p h (g j u) -> p (h g) j u", g=2, u=2)
-            nc.vector.tensor_copy(out=perm[:].rearrange("p r u j -> p r j u"), in_=src)
-            ordered[unit] = [[perm[:, 2 * h + q // 2, q % 2, :] for q in range(4)] for h in range(2)]
+                rows = im_w[:, unit[1], :, :].rearrange("p r (s w) -> p (r s) w", s=2)
+                nc.vector.tensor_copy(
+                    out=perm[:].rearrange("p u r j -> p r j u"), in_=rows.rearrange("p r (j u) -> p r j u", u=2),
+                )
+            ordered[unit] = perm
 
-        def every_2nd(unit):
-            if unit[0] == "Y":
-                c, g = unit[1:]
-                return [
-                    [ybr_w[:, 4 * c + 2 * h + q // 2, 256 * g + q % 2:256 * g + 256:2] for q in range(4)] for h in range(2)
-                ]
+        def words(unit, row, s, u):
+            if unit in ordered:
+                return ordered[unit][:, u, row if unit[0] == "Y" else 2 * row + s, :]
             rows = im_w[:, unit[1], :, :] if unit[0] == "I" else volt_w[:, 2 * unit[1]:2 * unit[1] + 2, :]
-            return [
-                [rows[:, h, 256 * (q // 2) + q % 2:256 * (q // 2) + 256:2] for q in range(4)] for h in range(2)
-            ]
+            return rows[:, row, 256 * s + u:256 * s + 256:2]
 
         def quantise(codes, scales, lo, words, src):
             def go():
@@ -156,28 +159,38 @@ def tile_pinnlayer_pa_kernel(tc, Volt, IM, Ybr, n_o_mu_i_u, out):
                 go()
 
         def turn(unit):
-            srcs = ordered[unit] if unit in ordered else every_2nd(unit)
-            if unit[0] == "I":
-                codes, scales, lo = icodes, iscales, 512 * unit[1]
-            elif unit[0] == "V":
-                codes, scales, lo = vcodes, vscales, 512 * unit[1]
-            else:
-                codes, scales, lo = ycodes, yscales, L2 * unit[2] + 512 * unit[1]
             grouped = stage.tile([P, 2, 1024], BF16, name="grouped", align_bytes=64)
             gw = grouped[:].bitcast(F32)
             banks = []
             for h in range(2):
                 bank = psum.tile([P, 512], F32, name="bank")
                 banks.append(bank)
+            pieces = []
+            for h in range(2):
                 for q in range(4):
-                    nc.tensor.transpose(bank[:, 128 * q:128 * q + 128], srcs[h][q], ident[:])
+                    if unit[0] == "I":
+                        pieces.append((q // 2, 2 * h + q % 2, words(unit, h, q // 2, q % 2), spread))
+                    elif unit[0] == "V":
+                        pieces.append((h, q, words(unit, h, q // 2, q % 2), ident))
+                    else:
+                        pieces.append((h, q, words(unit, 2 * h + q // 2, 0, q % 2), ident))
+            for to, place, src, moving in pieces:
+                nc.tensor.transpose(banks[to][:, 128 * place:128 * place + 128], src, moving[:])
+            if unit[0] == "I":
+                codes, scales, lo = icodes, iscales, 512 * unit[1]
+            elif unit[0] == "V":
+                codes, scales, lo = vcodes, vscales, 512 * unit[1]
+            else:
+                codes, scales, lo = ycodes, yscales, L2 * unit[2] + 512 * unit[1]
             count["turn"] += 1
             for h in ((1, 0) if count["turn"] > 2 else (0, 1)):
-                copy(
-                    "V" if h == 0 and count["turn"] > LEAD and count["turn"] % TURN_V == 0 else "S",
-                    gw[:, h, :].rearrange("p (s r u) -> p s r u", s=2, u=2),
-                    banks[h][:].rearrange("p (s u r) -> p s r u", s=2, u=2),
-                )
+                if unit[0] == "I":
+                    dst = gw[:, :, 256 * h:256 * h + 256].rearrange("p u (q x) -> p u q x", x=4)
+                    src = banks[h][:].rearrange("p (x u q) -> p u q x", x=4, u=2)
+                else:
+                    dst = gw[:, h, :].rearrange("p (s r u) -> p s r u", s=2, u=2)
+                    src = banks[h][:].rearrange("p (s u r) -> p s r u", s=2, u=2)
+                copy("V" if h == 0 and count["turn"] > LEAD and count["turn"] % TURN_V == 0 else "S", dst, src)
             quantise(codes, scales, lo, 512, grouped[:].rearrange("p h c -> p (h c)"))
 
         def first_matmul(g2, half):
@@ -190,7 +203,7 @@ def tile_pinnlayer_pa_kernel(tc, Volt, IM, Ybr, n_o_mu_i_u, out):
                     banks.append(bank)
                     for t in range(4):
                         for g in range(2):
-                            wi = 256 * (4 * g2 + t) + 128 * g
+                            wi = 512 * (2 * g2 + t % 2) + 256 * (t // 2) + 128 * g
                             wv = 256 * j + 128 * g
                             nc.tensor.matmul_mx(
                                 out=bank[:, 128 * t:128 * t + 128],

@@ -19,15 +19,16 @@ JB = B // P
 FLOPS = 2 * B * N2 * L2 + 2 * B * L2 * L2
 LEAD = 6
 RUNS = ((1, 3), (1, 3), (1, 3), (1, 2), (1, 2), (1, 0))
-TURN_V = 4
-DIRECT = 7
+TURN_V = 3
+DIRECT = 6
 AHEAD = 3
 ABS_TILES = [(j, 1) for j in range(0, 8, 2)]
 MU_END = 20
 FINE = 5
 LAST = (0, 256, 512, 768)
 FA, FW = 2, 3
-MU_A = {19: (-1,), 20: (0,), 21: (-2, 1), 22: (2,)}
+ABS_MU = {19: 0, 21: 1}
+SUM_MU = {20: 0, 21: 1, 22: 2}
 MU_AT = {q: 3 * q - 6 for q in range(3, 8)}
 
 
@@ -60,7 +61,7 @@ def tile_pinnlayer_pa_kernel(tc, Volt, IM, Ybr, n_o_mu_i_u, out):
         make_identity(nc, ident[:])
         spread = keep.tile([P, P], F32, name="spread")
         nc.vector.tensor_copy(
-            out=spread[:].rearrange("p (u q) -> p u q", u=2), in_=ident[:].rearrange("p (q u) -> p u q", u=2),
+            out=spread[:].rearrange("p (u m i) -> p u m i", u=2, i=4), in_=ident[:].rearrange("p (m u i) -> p u m i", u=2, i=4),
         )
 
         volt_sb = keep.tile([P, JB, N2], BF16, name="volt_sb")
@@ -123,25 +124,26 @@ def tile_pinnlayer_pa_kernel(tc, Volt, IM, Ybr, n_o_mu_i_u, out):
                 nc.scalar.copy(out=dst, in_=src)
 
         def put_in_order(unit):
-            perm = stage.tile([P, 2, 4, 128], F32, name="perm", align_bytes=64)
             if unit[0] == "Y":
-                c, g = unit[1:]
-                rows = ybr_w[:, 4 * c:4 * c + 4, 256 * g:256 * g + 256]
-                pairs = rows.rearrange("p r (q u b) -> p u r q b", u=2, b=2)
-                for u in range(2):
-                    nc.vector.tensor_copy(
-                        out=perm[:, u, :, :].rearrange("p r (q b) -> p r q b", b=2), in_=pairs[:, u, :, :, :],
-                    )
-            else:
-                rows = im_w[:, unit[1], :, :].rearrange("p r (s w) -> p (r s) w", s=2)
-                nc.vector.tensor_copy(
-                    out=perm[:].rearrange("p u r j -> p r j u"), in_=rows.rearrange("p r (j u) -> p r j u", u=2),
-                )
+                c, h = unit[1:]
+                eight = stage.tile([P, 2, 6, 128], F32, name="eight", align_bytes=64, bufs=4)
+                src = ybr_w[:, 4 * c + 2 * h:4 * c + 2 * h + 2, :].rearrange("p r (n u b) -> p u (r n) b", u=2, b=8)
+                nc.vector.tensor_copy(out=eight[:].rearrange("p u n (m b) -> p u (n m) b", b=8), in_=src)
+                ordered[unit] = eight
+                return
+            perm = stage.tile([P, 2, 4, 128], F32, name="perm", align_bytes=64, bufs=3)
+            rows = im_w[:, unit[1], :, :].rearrange("p r (s w) -> p (r s) w", s=2)
+            nc.vector.tensor_copy(
+                out=perm[:].rearrange("p u r j -> p r j u"), in_=rows.rearrange("p r (j u) -> p r j u", u=2),
+            )
             ordered[unit] = perm
 
         def words(unit, row, s, u):
+            if unit[0] == "Y":
+                c, g = unit[1:]
+                return ordered[("Y", c, row // 2)][:, u, 3 * (row % 2) + g, :]
             if unit in ordered:
-                return ordered[unit][:, u, row if unit[0] == "Y" else 2 * row + s, :]
+                return ordered[unit][:, u, 2 * row + s, :]
             rows = im_w[:, unit[1], :, :] if unit[0] == "I" else volt_w[:, 2 * unit[1]:2 * unit[1] + 2, :]
             return rows[:, row, 256 * s + u:256 * s + 256:2]
 
@@ -190,7 +192,7 @@ def tile_pinnlayer_pa_kernel(tc, Volt, IM, Ybr, n_o_mu_i_u, out):
                 else:
                     dst = gw[:, h, :].rearrange("p (s r u) -> p s r u", s=2, u=2)
                     src = banks[h][:].rearrange("p (s u r) -> p s r u", s=2, u=2)
-                copy("V" if h == 0 and count["turn"] > LEAD and count["turn"] % TURN_V == 0 else "S", dst, src)
+                copy("V" if h == 0 and count["turn"] > LEAD and count["turn"] % TURN_V == 1 else "S", dst, src)
             quantise(codes, scales, lo, 512, grouped[:].rearrange("p h c -> p (h c)"))
 
         def first_matmul(g2, half):
@@ -235,23 +237,29 @@ def tile_pinnlayer_pa_kernel(tc, Volt, IM, Ybr, n_o_mu_i_u, out):
             )
 
         turns, order = unit_order()
+        put_after = {}
+        for i in range(DIRECT, len(turns)):
+            if turns[i][0] == "I":
+                put_after.setdefault(i - AHEAD, []).append(turns[i])
+            elif turns[i][2] == 0:
+                for h in range(2):
+                    put_after.setdefault(i - AHEAD - 1 + h, []).append(("Y", turns[i][1], h))
         at = 0
         for n, unit in enumerate(order):
             if unit[0] == "S":
                 flush(1)
                 first_matmul(unit[1], unit[2])
             else:
-                ahead = at + AHEAD
                 at += 1
                 turn(unit)
             flush(1)
-            if unit[0] != "S" and DIRECT <= ahead < len(turns):
-                put_in_order(turns[ahead])
-            for j in MU_A.get(n, ()):
-                if j < 0:
-                    abs_mu(-1 - j)
-                else:
-                    sum_mu(j)
+            if unit[0] != "S":
+                for part in put_after.get(at - 1, ()):
+                    put_in_order(part)
+            if n in ABS_MU:
+                abs_mu(ABS_MU[n])
+            if n in SUM_MU:
+                sum_mu(SUM_MU[n])
         flush(0)
 
         im_free = im_w.rearrange("p t h w -> p (t h w)")
@@ -276,7 +284,7 @@ def tile_pinnlayer_pa_kernel(tc, Volt, IM, Ybr, n_o_mu_i_u, out):
 
         def square(j, lo, hi, col, bank):
             if j not in sqs:
-                sqs[j] = epi.tile([P, 2, L], F32, name="sq", bufs=3)
+                sqs[j] = ybr_w[:, 2 * (j % 6):2 * (j % 6) + 2, :]
             w = hi - lo
             nc.scalar.activation(
                 out=sqs[j][:, :, lo:hi], in_=bank[:, 0:2 * w].rearrange("p (a w) -> p a w", a=2), func=ACT.Square,

@@ -57,27 +57,27 @@ def tile_pinnlayer_pa_kernel(tc, Volt, IM, Ybr, n_o_mu_i_u, out):
         epi = ctx.enter_context(tc.tile_pool(name="epi", bufs=4))
         psum = ctx.enter_context(tc.psum_pool(name="psum", bufs=8))
 
-        ident = keep.tile([P, P], F32, name="ident")
+        ident = keep.tile([P, P], F32, name="ident", align_bytes=256)
         make_identity(nc, ident[:])
-        spread = keep.tile([P, P], F32, name="spread")
+        spread = keep.tile([P, P], F32, name="spread", align_bytes=256)
         nc.vector.tensor_copy(
             out=spread[:].rearrange("p (u m i) -> p u m i", u=2, i=4), in_=ident[:].rearrange("p (m u i) -> p u m i", u=2, i=4),
         )
 
-        volt_sb = keep.tile([P, JB, N2], BF16, name="volt_sb")
-        im_sb = keep.tile([P, 6, 2, N2], BF16, name="im_sb")
+        volt_sb = keep.tile([P, JB, N2], BF16, name="volt_sb", align_bytes=256)
+        im_sb = keep.tile([P, 6, 2, N2], BF16, name="im_sb", align_bytes=256)
         ybr_sb = keep.tile([P, 12, L2], BF16, name="ybr_sb")
         mu_sb = keep.tile([P, JB, L], BF16, name="mu_sb")
         a_sb = keep.tile([P, JB, L], BF16, name="a_sb")
 
-        vcodes = keep.tile([P, JB * 256], U32, name="vcodes", align_bytes=64)
-        vscales = keep.tile([P, JB * 256], U8, name="vscales", align_bytes=64)
-        icodes = keep.tile([P, 12 * 256], U32, name="icodes", align_bytes=64)
-        iscales = keep.tile([P, 12 * 256], U8, name="iscales", align_bytes=64)
-        ycodes = keep.tile([P, 3 * L2], U32, name="ycodes", align_bytes=64)
-        yscales = keep.tile([P, 3 * L2], U8, name="yscales", align_bytes=64)
-        dcodes = keep.tile([P, 3 * B], U32, name="dcodes", align_bytes=64)
-        dscales = keep.tile([P, 3 * B], U8, name="dscales", align_bytes=64)
+        vcodes = keep.tile([P, JB * 256], U32, name="vcodes", align_bytes=256)
+        vscales = keep.tile([P, JB * 256], U8, name="vscales", align_bytes=256)
+        icodes = keep.tile([P, 12 * 256], U32, name="icodes", align_bytes=256)
+        iscales = keep.tile([P, 12 * 256], U8, name="iscales", align_bytes=256)
+        ycodes = keep.tile([P, 3 * L2], U32, name="ycodes", align_bytes=256)
+        yscales = keep.tile([P, 3 * L2], U8, name="yscales", align_bytes=256)
+        dcodes = keep.tile([P, 3 * B], U32, name="dcodes", align_bytes=256)
+        dscales = keep.tile([P, 3 * B], U8, name="dscales", align_bytes=256)
 
         halves = keep.tile([P, JB, 9], F32, name="halves")
         wholes = keep.tile([P, JB, 4], F32, name="wholes")
@@ -126,12 +126,12 @@ def tile_pinnlayer_pa_kernel(tc, Volt, IM, Ybr, n_o_mu_i_u, out):
         def put_in_order(unit):
             if unit[0] == "Y":
                 c, h = unit[1:]
-                eight = stage.tile([P, 2, 6, 128], F32, name="eight", align_bytes=64, bufs=4)
+                eight = stage.tile([P, 2, 6, 128], F32, name="eight", align_bytes=256, bufs=4)
                 src = ybr_w[:, 4 * c + 2 * h:4 * c + 2 * h + 2, :].rearrange("p r (n u b) -> p u (r n) b", u=2, b=8)
                 nc.vector.tensor_copy(out=eight[:].rearrange("p u n (m b) -> p u (n m) b", b=8), in_=src)
                 ordered[unit] = eight
                 return
-            perm = stage.tile([P, 2, 4, 128], F32, name="perm", align_bytes=64, bufs=3)
+            perm = stage.tile([P, 2, 4, 128], F32, name="perm", align_bytes=256, bufs=3)
             rows = im_w[:, unit[1], :, :].rearrange("p r (s w) -> p (r s) w", s=2)
             nc.vector.tensor_copy(
                 out=perm[:].rearrange("p u r j -> p r j u"), in_=rows.rearrange("p r (j u) -> p r j u", u=2),
@@ -161,7 +161,7 @@ def tile_pinnlayer_pa_kernel(tc, Volt, IM, Ybr, n_o_mu_i_u, out):
                 go()
 
         def turn(unit):
-            grouped = stage.tile([P, 2, 1024], BF16, name="grouped", align_bytes=64)
+            grouped = stage.tile([P, 2, 1024], BF16, name="grouped", align_bytes=256)
             gw = grouped[:].bitcast(F32)
             banks = []
             for h in range(2):
@@ -196,7 +196,7 @@ def tile_pinnlayer_pa_kernel(tc, Volt, IM, Ybr, n_o_mu_i_u, out):
             quantise(codes, scales, lo, 512, grouped[:].rearrange("p h c -> p (h c)"))
 
         def first_matmul(g2, half):
-            dgrp = stage.tile([P, 4, 512], BF16, name="dgrp", align_bytes=64, bufs=2)
+            dgrp = stage.tile([P, 4, 512], BF16, name="dgrp", align_bytes=256, bufs=2)
             for pair in range(2):
                 banks = []
                 for h in range(2):

from contextlib import ExitStack

import concourse.mybir as mybir
from concourse.masks import make_identity

F32 = mybir.dt.float32
BF16 = mybir.dt.bfloat16
U32 = mybir.dt.uint32
U8 = mybir.dt.uint8
I32 = mybir.dt.int32
FP8X4 = mybir.dt.float8_e4m3fn_x4
ALU = mybir.AluOpType
ACT = mybir.ActivationFunctionType
AX = mybir.AxisListType

P = 128
B, N2, L2, L = 1024, 1024, 1536, 768
JB = B // P
FLOPS = 2 * B * N2 * L2 + 2 * B * L2 * L2
LEAD = 6
RUNS = ((1, 3), (1, 3), (1, 3), (1, 2), (1, 2), (1, 0))
TURN_V = 3
DIRECT = 6
AHEAD = 3
ABS_TILES = [(j, 1) for j in range(0, 8, 2)]
MU_END = 20
FINE = 5
LAST = (0, 256, 512, 768)
FA, FW = 2, 3
ABS_MU = {19: 0, 21: 1}
SUM_MU = {20: 0, 21: 1, 22: 2}
MU_AT = {q: 3 * q - 6 for q in range(3, 8)}


def unit_order():
    turns = [("I", 0), ("I", 1)] + [("V", c) for c in range(4)] + [("I", t) for t in range(2, 6)]
    turns = turns + [("Y", c, g) for c in range(3) for g in range(3)]
    first = [("S", g, q) for g in range(3) for q in range(2)]
    order = turns[:LEAD]
    done = LEAD
    at = 0
    for mx, run in RUNS:
        order = order + first[at:at + mx] + turns[done:done + run]
        at += mx
        done += run
    assert at == len(first)
    assert done == len(turns)
    return turns, order


def tile_pinnlayer_pa_kernel(tc, Volt, IM, Ybr, n_o_mu_i_u, out):
    nc = tc.nc
    with ExitStack() as ctx:
        ctx.enter_context(tc.manual_schedule())
        keep = ctx.enter_context(tc.tile_pool(name="keep", bufs=1))
        stage = ctx.enter_context(tc.tile_pool(name="stage", bufs=4))
        epi = ctx.enter_context(tc.tile_pool(name="epi", bufs=4))
        psum = ctx.enter_context(tc.psum_pool(name="psum", bufs=8))

        ident = keep.tile([P, P], F32, name="ident", align_bytes=256)
        make_identity(nc, ident[:])
        spread = keep.tile([P, P], F32, name="spread", align_bytes=256)
        nc.vector.tensor_copy(
            out=spread[:].rearrange("p (u m i) -> p u m i", u=2, i=4), in_=ident[:].rearrange("p (m u i) -> p u m i", u=2, i=4),
        )

        volt_sb = keep.tile([P, JB, N2], BF16, name="volt_sb", align_bytes=256)
        im_sb = keep.tile([P, 6, 2, N2], BF16, name="im_sb", align_bytes=256)
        ybr_sb = keep.tile([P, 12, L2], BF16, name="ybr_sb")
        mu_sb = keep.tile([P, JB, L], BF16, name="mu_sb")
        a_sb = keep.tile([P, JB, L], BF16, name="a_sb")

        vcodes = keep.tile([P, JB * 256], U32, name="vcodes", align_bytes=256)
        vscales = keep.tile([P, JB * 256], U8, name="vscales", align_bytes=256)
        icodes = keep.tile([P, 12 * 256], U32, name="icodes", align_bytes=256)
        iscales = keep.tile([P, 12 * 256], U8, name="iscales", align_bytes=256)
        ycodes = keep.tile([P, 3 * L2], U32, name="ycodes", align_bytes=256)
        yscales = keep.tile([P, 3 * L2], U8, name="yscales", align_bytes=256)
        dcodes = keep.tile([P, 3 * B], U32, name="dcodes", align_bytes=256)
        dscales = keep.tile([P, 3 * B], U8, name="dscales", align_bytes=256)

        halves = keep.tile([P, JB, 9], F32, name="halves")
        wholes = keep.tile([P, JB, 4], F32, name="wholes")
        acc_m = keep.tile([P, JB], F32, name="acc_m")
        warm = keep.tile([P, 1], F32, name="warm")
        nc.vector.memset(warm[:], 0.0)
        nc.vector.memset(halves[:], 0.0)
        nc.vector.memset(wholes[:], 0.0)
        nc.scalar.activation(out=warm[:], in_=warm[:], func=ACT.Abs)

        volt_v = Volt.rearrange("(p j) k -> p j k", j=JB)
        im_v = IM.rearrange("(g p r e) k -> p g e r k", g=3, r=2, e=2)
        ybr_v = Ybr.rearrange("(r p) k -> p r k", p=P)
        mu_v = n_o_mu_i_u.rearrange("(p j) l -> p j l", j=JB)

        def load_im(t, lo, hi):
            nc.sync.dma_start(out=im_sb[:, t, lo:hi, :], in_=im_v[:, t // 2, t % 2, lo:hi, :])

        load_im(0, 0, 1)
        load_im(0, 1, 2)
        load_im(1, 0, 2)
        for c in range(4):
            nc.sync.dma_start(out=volt_sb[:, 2 * c:2 * c + 2, :], in_=volt_v[:, 2 * c:2 * c + 2, :])
        for t in range(2, 6):
            load_im(t, 0, 2)
        for rp in (0, 3, 1, 4, 2, 5):
            at = 4 * (rp % 3) + 2 * (rp // 3)
            nc.sync.dma_start(out=ybr_sb[:, at:at + 2, :], in_=ybr_v[:, 2 * rp:2 * rp + 2, :])
        for h in range(2):
            nc.sync.dma_start(out=mu_sb[:, 4 * h:4 * h + 4, :], in_=mu_v[:, 4 * h:4 * h + 4, :])

        volt_w = volt_sb[:].bitcast(F32)
        im_w = im_sb[:].bitcast(F32)
        ybr_w = ybr_sb[:].bitcast(F32)

        count = {"turn": 0}
        late = []
        ordered = {}

        def copy(eng, dst, src):
            if eng == "V":
                nc.vector.tensor_copy(out=dst, in_=src)
            else:
                nc.scalar.copy(out=dst, in_=src)

        def put_in_order(unit):
            if unit[0] == "Y":
                c, h = unit[1:]
                eight = stage.tile([P, 2, 6, 128], F32, name="eight", align_bytes=256, bufs=4)
                src = ybr_w[:, 4 * c + 2 * h:4 * c + 2 * h + 2, :].rearrange("p r (n u b) -> p u (r n) b", u=2, b=8)
                nc.vector.tensor_copy(out=eight[:].rearrange("p u n (m b) -> p u (n m) b", b=8), in_=src)
                ordered[unit] = eight
                return
            perm = stage.tile([P, 2, 4, 128], F32, name="perm", align_bytes=256, bufs=3)
            rows = im_w[:, unit[1], :, :].rearrange("p r (s w) -> p (r s) w", s=2)
            nc.vector.tensor_copy(
                out=perm[:].rearrange("p u r j -> p r j u"), in_=rows.rearrange("p r (j u) -> p r j u", u=2),
            )
            ordered[unit] = perm

        def words(unit, row, s, u):
            if unit[0] == "Y":
                c, g = unit[1:]
                return ordered[("Y", c, row // 2)][:, u, 3 * (row % 2) + g, :]
            if unit in ordered:
                return ordered[unit][:, u, 2 * row + s, :]
            rows = im_w[:, unit[1], :, :] if unit[0] == "I" else volt_w[:, 2 * unit[1]:2 * unit[1] + 2, :]
            return rows[:, row, 256 * s + u:256 * s + 256:2]

        def quantise(codes, scales, lo, words, src):
            def go():
                nc.vector.quantize_mx(
                    out=codes[:, lo:lo + words].bitcast(FP8X4), scales=scales[:, lo:lo + words], in_=src,
                )
            late.append(go)

        def flush(left):
            while len(late) > left:
                go = late[0]
                late.remove(go)
                go()

        def turn(unit):
            grouped = stage.tile([P, 2, 1024], BF16, name="grouped", align_bytes=256)
            gw = grouped[:].bitcast(F32)
            banks = []
            for h in range(2):
                bank = psum.tile([P, 512], F32, name="bank")
                banks.append(bank)
            pieces = []
            for h in range(2):
                for q in range(4):
                    if unit[0] == "I":
                        pieces.append((q // 2, 2 * h + q % 2, words(unit, h, q // 2, q % 2), spread))
                    elif unit[0] == "V":
                        pieces.append((h, q, words(unit, h, q // 2, q % 2), ident))
                    else:
                        pieces.append((h, q, words(unit, 2 * h + q // 2, 0, q % 2), ident))
            for to, place, src, moving in pieces:
                nc.tensor.transpose(banks[to][:, 128 * place:128 * place + 128], src, moving[:])
            if unit[0] == "I":
                codes, scales, lo = icodes, iscales, 512 * unit[1]
            elif unit[0] == "V":
                codes, scales, lo = vcodes, vscales, 512 * unit[1]
            else:
                codes, scales, lo = ycodes, yscales, L2 * unit[2] + 512 * unit[1]
            count["turn"] += 1
            for h in ((1, 0) if count["turn"] > 2 else (0, 1)):
                if unit[0] == "I":
                    dst = gw[:, :, 256 * h:256 * h + 256].rearrange("p u (q x) -> p u q x", x=4)
                    src = banks[h][:].rearrange("p (x u q) -> p u q x", x=4, u=2)
                else:
                    dst = gw[:, h, :].rearrange("p (s r u) -> p s r u", s=2, u=2)
                    src = banks[h][:].rearrange("p (s u r) -> p s r u", s=2, u=2)
                copy("V" if h == 0 and count["turn"] > LEAD and count["turn"] % TURN_V == 1 else "S", dst, src)
            quantise(codes, scales, lo, 512, grouped[:].rearrange("p h c -> p (h c)"))

        def first_matmul(g2, half):
            dgrp = stage.tile([P, 4, 512], BF16, name="dgrp", align_bytes=256, bufs=2)
            for pair in range(2):
                banks = []
                for h in range(2):
                    j = 4 * half + 2 * pair + h
                    bank = psum.tile([P, 512], F32, name="bank")
                    banks.append(bank)
                    for t in range(4):
                        for g in range(2):
                            wi = 512 * (2 * g2 + t % 2) + 256 * (t // 2) + 128 * g
                            wv = 256 * j + 128 * g
                            nc.tensor.matmul_mx(
                                out=bank[:, 128 * t:128 * t + 128],
                                lhsT=icodes[:, wi:wi + 128].bitcast(FP8X4), lhsT_scale=iscales[:, wi:wi + 128],
                                rhs=vcodes[:, wv:wv + 128].bitcast(FP8X4), rhs_scale=vscales[:, wv:wv + 128],
                                start=(g == 0), stop=(g == 1),
                            )
                for h in (1, 0):
                    copy(
                        "S",
                        dgrp[:, 2 * pair + h, :].rearrange("p (b t) -> p b t", t=4),
                        banks[h][:].rearrange("p (t b) -> p b t", t=4),
                    )
                if pair == 0:
                    flush(0)
            quantise(dcodes, dscales, B * g2 + 512 * half, 512, dgrp[:].rearrange("p h c -> p (h c)"))

        def sum_mu(j):
            junk_m = epi.tile([P, L // 2], F32, name="junk_m", bufs=2)
            nc.vector.scalar_tensor_tensor(
                out=junk_m[:], in0=mu_sb[:, j, 0:L // 2], scalar=0.0, in1=mu_sb[:, j, L // 2:L],
                op0=ALU.add, op1=ALU.add, accum_out=acc_m[:, j:j + 1],
            )

        def abs_mu(h):
            nc.vector.tensor_single_scalar(
                out=a_sb[:, 4 * h:4 * h + 4, :].bitcast(I32), in_=mu_sb[:, 4 * h:4 * h + 4, :].bitcast(I32),
                scalar=0x7FFF7FFF, op=ALU.bitwise_and,
            )

        turns, order = unit_order()
        put_after = {}
        for i in range(DIRECT, len(turns)):
            if turns[i][0] == "I":
                put_after.setdefault(i - AHEAD, []).append(turns[i])
            elif turns[i][2] == 0:
                for h in range(2):
                    put_after.setdefault(i - AHEAD - 1 + h, []).append(("Y", turns[i][1], h))
        at = 0
        for n, unit in enumerate(order):
            if unit[0] == "S":
                flush(1)
                first_matmul(unit[1], unit[2])
            else:
                at += 1
                turn(unit)
            flush(1)
            if unit[0] != "S":
                for part in put_after.get(at - 1, ()):
                    put_in_order(part)
            if n in ABS_MU:
                abs_mu(ABS_MU[n])
            if n in SUM_MU:
                sum_mu(SUM_MU[n])
        flush(0)

        im_free = im_w.rearrange("p t h w -> p (t h w)")
        volt_free = volt_w.rearrange("p j w -> p (j w)")
        xs, zs, sqs = {}, {}, {}

        def currents(j, lo, hi):
            c, off, width = lo // 256, lo % 256, hi - lo
            bank = psum.tile([P, 512], F32, name="bank")
            parts = [(0, off, 512)] if width == 256 else [(0, off, width), (width, 256 + off, width)]
            for to, fro, n in parts:
                for g in range(3):
                    wd = B * g + 128 * j
                    wy = L2 * g + 512 * c + fro
                    nc.tensor.matmul_mx(
                        out=bank[:, to:to + n],
                        lhsT=dcodes[:, wd:wd + 128].bitcast(FP8X4), lhsT_scale=dscales[:, wd:wd + 128],
                        rhs=ycodes[:, wy:wy + n].bitcast(FP8X4), rhs_scale=yscales[:, wy:wy + n],
                        start=(g == 0), stop=(g == 2),
                    )
            return bank

        def square(j, lo, hi, col, bank):
            if j not in sqs:
                sqs[j] = ybr_w[:, 2 * (j % 6):2 * (j % 6) + 2, :]
            w = hi - lo
            nc.scalar.activation(
                out=sqs[j][:, :, lo:hi], in_=bank[:, 0:2 * w].rearrange("p (a w) -> p a w", a=2), func=ACT.Square,
                accum_out=halves[:, j, col:col + 1],
            )

        def make_x(j, lo, hi):
            if lo == 0:
                xs[j] = im_free[:, L * (j % 4):L * (j % 4) + L]
            nc.vector.scalar_tensor_tensor(
                out=xs[j][:, lo:hi], in0=sqs[j][:, 0, lo:hi], scalar=-1.0, in1=sqs[j][:, 1, lo:hi], op0=ALU.add, op1=ALU.add,
            )

        def make_abs(j, lo, hi, col):
            if lo == 0:
                zs[j] = im_free[:, L * (4 + j % 4):L * (5 + j % 4)]
            x, z = xs[j], zs[j]
            if (j, col) in ABS_TILES:
                nc.vector.scalar_tensor_tensor(
                    out=z[:, lo:hi], in0=x[:, lo:hi], scalar=-1.0, in1=x[:, lo:hi], op0=ALU.mult, op1=ALU.max,
                    accum_out=halves[:, j, 4 + col:5 + col],
                )
            else:
                nc.scalar.activation(out=z[:, lo:hi], in_=x[:, lo:hi], func=ACT.Abs, accum_out=halves[:, j, 4 + col:5 + col])

        def weigh(j, lo, hi, col):
            junk_w = volt_free[:, L * (j % 4):L * (j % 4) + L]
            nc.vector.scalar_tensor_tensor(
                out=junk_w[:, lo:hi], in0=zs[j][:, lo:hi], scalar=0.5, in1=a_sb[:, j, lo:hi],
                op0=ALU.add, op1=ALU.mult, accum_out=wholes[:, j, col:col + 1],
            )


        todo = {}

        def after(s, f, *args):
            todo.setdefault(s, []).append((f, args))

        steps = []
        for j in range(JB):
            cuts = LAST if j == JB - 1 else (0, 256, 512, 768)
            for c in range(len(cuts) - 1):
                steps.append((j, cuts[c], cuts[c + 1], c))
        for s in range(len(steps)):
            j, lo, hi, c = steps[s]
            after(s, make_x, j, lo, hi)
            after(s + FA, make_abs, j, lo, hi, c)
            if j >= FINE:
                after(s + FW, weigh, j, lo, hi, c)
            elif c == 2:
                after(s + FW, weigh, j, 0, L, 0)
        for q in range(JB):
            if q in MU_AT:
                after(MU_AT[q], sum_mu, q)
        for s in range(len(steps) + 4):
            if s < len(steps):
                j, lo, hi, c = steps[s]
                square(j, lo, hi, c, currents(j, lo, hi))
            for f, args in todo.get(s, ()):
                f(*args)
            if s == MU_END:
                nc.vector.tensor_scalar(
                    out=halves[:, :, 8], in0=acc_m[:], scalar1=-1.0, scalar2=-1.0 * L, op0=ALU.mult, op1=ALU.add,
                )

        twice = keep.tile([P, JB], F32, name="twice")
        nc.vector.tensor_reduce(out=twice[:], in_=halves[:], axis=AX.X, op=ALU.add)
        whole = keep.tile([P, JB], F32, name="whole")
        nc.vector.tensor_reduce(out=whole[:], in_=wholes[:], axis=AX.X, op=ALU.add)
        res = keep.tile([P, JB], F32, name="res")
        nc.vector.scalar_tensor_tensor(
            out=res[:], in0=twice[:], scalar=0.5, in1=whole[:], op0=ALU.mult, op1=ALU.add,
        )
        nc.sync.dma_start(out=out.rearrange("(p j) -> p j", j=JB), in_=res[:])
